import numpy as np
import ml_dtypes


def mxq(x, axis, fmt="e4m3"):
    dtype, down = {"e4m3": (ml_dtypes.float8_e4m3fn, 7), "e5m2": (ml_dtypes.float8_e5m2, 14)}[fmt]
    v = np.moveaxis(np.asarray(x, np.float32).astype(ml_dtypes.bfloat16).astype(np.float64), axis, -1)
    blocks = v.reshape(v.shape[:-1] + (-1, 32))
    amax = np.abs(blocks).max(-1, keepdims=True)
    byte = np.maximum(np.where(amax > 0, np.frexp(amax)[1] - 1 + 127, 0) - down, 1)
    scale = np.exp2(byte - 127.0)
    codes = (blocks / scale).astype(np.float32).astype(dtype).astype(np.float64)
    return np.moveaxis((codes * scale).reshape(v.shape), -1, axis)


WIDE = False


def mx_kscale(k):
    if not WIDE:
        return np.ones(k)
    levels = np.array([10, -10, 5, -5, 0])
    a = np.random.permutation(np.resize(levels, k // 512 * 4)).reshape(k // 512, 4)
    idx = np.arange(k)
    return np.exp2(a[idx // 512, idx % 128 // 32])


BF16 = ml_dtypes.bfloat16


def bf(x):
    return np.asarray(x, np.float32).astype(BF16)


def f64(x):
    return np.asarray(x).astype(np.float64)


B, N, D, E = 2, 512, 16384, 128

EPS = 1e-6
NUM_ITERS = 8
TEMPERATURE = 1.0
FRAC = 0.7
SEP = 2.0


def logsumexp(t, axis):
    m = t.max(axis=axis, keepdims=True)
    return m + np.log(np.exp(t - m).sum(axis=axis, keepdims=True))


def sinkhorn(t):
    t = np.log(np.maximum(t, EPS))
    t = t / TEMPERATURE
    for _ in range(NUM_ITERS):
        t = t - logsumexp(t, -2)
        t = t - logsumexp(t, -1)
    return np.exp(t)


def setup_inputs():
    s = mx_kscale(D)
    p = np.where(np.random.random(D) < 0.5, 1.0, -1.0)
    side = np.where(np.random.random((B, N, 1)) < FRAC, 1.0, -1.0)
    half = np.where(np.arange(E) < E // 2, 1.0, -1.0)[:, None]
    z = np.random.standard_normal((B, N, D))
    z = z - (z @ p)[..., None] * p / D
    g = np.random.standard_normal((E, D))
    g = g - (g @ p)[:, None] * p / D
    return {"x": bf((z + side * p) * s), "w_gate": bf((g / np.sqrt(D) + SEP * half * p / D) / s)}


def reference(x, w_gate):
    gates = mxq(f64(x), 2, "e4m3") @ mxq(f64(w_gate), 1, "e4m3").T
    return sinkhorn(gates)

@@ -1,0 +1,233 @@
+from contextlib import ExitStack
+
+import concourse.mybir as mybir
+from concourse.masks import make_identity
+
+F32 = mybir.dt.float32
+BF16 = mybir.dt.bfloat16
+U32 = mybir.dt.uint32
+U8 = mybir.dt.uint8
+FP8X4 = mybir.dt.float8_e4m3fn_x4
+ALU = mybir.AluOpType
+
+P = 128
+PACK = 4
+K_PASS = P * PACK
+HALVES = 2
+BANK_WORDS = 512
+
+BATCH, TOKENS, D, EXPERTS = 2, 512, 16384, 128
+TILES_PER_BATCH = TOKENS // P
+TOKEN_TILES = BATCH * TILES_PER_BATCH
+EPS = 1e-6
+ROUNDS = 8
+
+SLICE_D = 4096
+SLICES = D // SLICE_D
+SLICE_PASSES = SLICE_D // K_PASS
+BANK_PASSES = BANK_WORDS // (HALVES * P)
+SLICE_BANKS = SLICE_PASSES // BANK_PASSES
+SLICE_COLS = SLICE_PASSES * P
+
+FLOPS = 2 * BATCH * TOKENS * D * EXPERTS
+
+
+def tile_sinkhornrouter_k_kernel(tc, x, w_gate, out):
+    nc = tc.nc
+    with ExitStack() as stack:
+        keep = stack.enter_context(tc.tile_pool(name="keep", bufs=1))
+        raw_pool = stack.enter_context(tc.tile_pool(name="raw", bufs=8))
+        grouped_pool = stack.enter_context(tc.tile_pool(name="grouped", bufs=3))
+        x_mx_pool = stack.enter_context(tc.tile_pool(name="x_mx", bufs=3))
+        vectors = stack.enter_context(tc.tile_pool(name="vectors", bufs=2))
+        banks = stack.enter_context(tc.psum_pool(name="banks", bufs=6))
+        gate_banks = stack.enter_context(tc.psum_pool(name="gate_banks", bufs=2))
+        stack.enter_context(tc.manual_schedule())
+
+        identity = keep.tile([P, P], F32, name="identity")
+        make_identity(nc, identity[:])
+        ones = keep.tile([P, 1], F32, name="ones")
+        nc.vector.memset(ones[:], 1.0)
+
+        w_codes = keep.tile([P, D // K_PASS * EXPERTS], U32, name="w_codes", align_bytes=64)
+        w_scales = keep.tile([P, D // K_PASS * EXPERTS], U8, name="w_scales", align_bytes=64)
+
+        k_by_expert = [keep.tile([P, TOKENS], F32, name="k_by_expert%d" % b) for b in range(BATCH)]
+        tile_sums = [keep.tile([P, TILES_PER_BATCH], F32, name="tile_sums%d" % b) for b in range(BATCH)]
+        kn_by_expert = [keep.tile([P, TOKENS], F32, name="kn_by_expert%d" % b) for b in range(BATCH)]
+        kn_by_token = [keep.tile([P, TOKENS], F32, name="kn_by_token%d" % b) for b in range(BATCH)]
+
+        token_rows = [
+            x[j // TILES_PER_BATCH].rearrange("(r c) d -> c r d", c=TILES_PER_BATCH)[j % TILES_PER_BATCH]
+            for j in range(TOKEN_TILES)
+        ]
+
+        slices = []
+        for s in range(SLICES):
+            slices.append((w_gate, None, s))
+            slices.append((token_rows[0], 0, s))
+        for j in range(1, TOKEN_TILES):
+            for s in range(SLICES):
+                slices.append((token_rows[j], j, s))
+
+        grouped_of = {}
+        mx_of = {}
+        gates_of = {}
+
+        def transpose_slice(i):
+            rows, j, s = slices[i]
+            raw = raw_pool.tile([P, SLICE_D], BF16, name="raw")
+            nc.sync.dma_start(out=raw[:], in_=rows[:, s * SLICE_D : (s + 1) * SLICE_D])
+            raw_words = raw[:].bitcast(F32)
+            grouped = grouped_pool.tile([P, SLICE_D], BF16, name="grouped", align_bytes=64)
+            grouped_words = grouped[:].bitcast(F32).rearrange(
+                "p (g r u) -> p g r u", g=SLICE_PASSES, u=HALVES
+            )
+            for k in range(SLICE_BANKS):
+                bank = banks.tile([P, BANK_WORDS], F32, name="bank")
+                for t in range(BANK_PASSES * HALVES):
+                    first = (k * BANK_PASSES * HALVES + t) * P
+                    nc.tensor.transpose(
+                        bank[:, t * P : (t + 1) * P], raw_words[:, first : first + P], identity[:]
+                    )
+                copy = nc.vector.tensor_copy if k == 0 else nc.scalar.copy
+                copy(
+                    out=grouped_words[:, k * BANK_PASSES : (k + 1) * BANK_PASSES, :, :],
+                    in_=bank[:].rearrange("p (g u r) -> p g r u", g=BANK_PASSES, u=HALVES),
+                )
+            grouped_of[i] = grouped
+
+        def quantise_slice(i):
+            rows, j, s = slices[i]
+            if j is None:
+                cols = slice(s * SLICE_COLS, (s + 1) * SLICE_COLS)
+                codes, scales = w_codes[:, cols], w_scales[:, cols]
+            else:
+                x_codes = x_mx_pool.tile([P, SLICE_COLS], U32, name="x_codes", align_bytes=64)
+                x_scales = x_mx_pool.tile([P, SLICE_COLS], U8, name="x_scales", align_bytes=64)
+                codes, scales = x_codes[:], x_scales[:]
+                mx_of[i] = (codes, scales)
+            nc.vector.quantize_mx(out=codes.bitcast(FP8X4), scales=scales, in_=grouped_of[i][:])
+
+        def multiply_slice(i):
+            rows, j, s = slices[i]
+            if j is None:
+                return
+            if s == 0:
+                gates_of[j] = gate_banks.tile([P, P], F32, name="gates")
+            gates = gates_of[j]
+            codes, scales = mx_of[i]
+            for g in range(SLICE_PASSES):
+                w_cols = slice((s * SLICE_PASSES + g) * P, (s * SLICE_PASSES + g + 1) * P)
+                x_cols = slice(g * P, (g + 1) * P)
+                nc.tensor.matmul_mx(
+                    out=gates[:],
+                    lhsT=w_codes[:, w_cols].bitcast(FP8X4),
+                    lhsT_scale=w_scales[:, w_cols],
+                    rhs=codes[:, x_cols].bitcast(FP8X4),
+                    rhs_scale=scales[:, x_cols],
+                    start=(s == 0 and g == 0),
+                    stop=(s == SLICES - 1 and g == SLICE_PASSES - 1),
+                )
+            if s == SLICES - 1:
+                clamp_tile(j)
+
+        def clamp_tile(j):
+            b, c = divmod(j, TILES_PER_BATCH)
+            nc.vector.tensor_scalar(
+                out=k_by_expert[b][:, c * P : (c + 1) * P],
+                in0=gates_of[j][:],
+                scalar1=EPS,
+                scalar2=None,
+                op0=ALU.max,
+                op1=ALU.add,
+                accum_out=tile_sums[b][:, c : c + 1],
+            )
+            if c == TILES_PER_BATCH - 1:
+                column_sum = vectors.tile([P, 1], F32, name="column_sum")
+                nc.vector.reduce_sum(out=column_sum[:], in_=tile_sums[b][:], axis=mybir.AxisListType.X)
+                first_v = vectors.tile([P, 1], F32, name="first_v")
+                nc.vector.reciprocal(out=first_v[:], in_=column_sum[:])
+                nc.vector.tensor_scalar(
+                    out=kn_by_expert[b][:],
+                    in0=k_by_expert[b][:],
+                    scalar1=first_v[:, 0:1],
+                    scalar2=None,
+                    op0=ALU.mult,
+                )
+
+        for i in range(len(slices) + 2):
+            if i < len(slices):
+                transpose_slice(i)
+            if 0 <= i - 1 < len(slices):
+                quantise_slice(i - 1)
+            if 0 <= i - 2:
+                multiply_slice(i - 2)
+
+        for b in range(BATCH):
+            bank = banks.tile([P, BANK_WORDS], F32, name="bank")
+            for c in range(TILES_PER_BATCH):
+                cols = slice(c * P, (c + 1) * P)
+                nc.tensor.transpose(bank[:, cols], kn_by_expert[b][:, cols], identity[:])
+            nc.scalar.copy(out=kn_by_token[b][:], in_=bank[:])
+
+        def expert_step(b, v):
+            bank = banks.tile([P, BANK_WORDS], F32, name="bank")
+            for c in range(TILES_PER_BATCH):
+                nc.tensor.matmul(
+                    out=bank[:, c : c + 1],
+                    lhsT=kn_by_expert[b][:, c * P : (c + 1) * P],
+                    rhs=v[:, 0:1],
+                    start=True,
+                    stop=True,
+                )
+            u = vectors.tile([P, TILES_PER_BATCH], F32, name="u%d" % b)
+            nc.vector.reciprocal(out=u[:], in_=bank[:, 0:TILES_PER_BATCH])
+            return u
+
+        def token_step(b, u):
+            bank = banks.tile([P, BANK_WORDS], F32, name="bank")
+            for c in range(TILES_PER_BATCH):
+                nc.tensor.matmul(
+                    out=bank[:, 0:1],
+                    lhsT=kn_by_token[b][:, c * P : (c + 1) * P],
+                    rhs=u[:, c : c + 1],
+                    start=(c == 0),
+                    stop=(c == TILES_PER_BATCH - 1),
+                )
+            v = vectors.tile([P, 1], F32, name="v%d" % b)
+            nc.vector.reciprocal(out=v[:], in_=bank[:, 0:1])
+            return v
+
+        v_of = [ones, ones]
+        u_of = [None, None]
+        for r in range(ROUNDS):
+            if r > 0:
+                for b in range(BATCH):
+                    v_of[b] = token_step(b, u_of[b])
+            for b in range(BATCH):
+                u_of[b] = expert_step(b, v_of[b])
+
+        for b in range(BATCH):
+            spread = banks.tile([P, BANK_WORDS], F32, name="bank")
+            nc.tensor.matmul(
+                out=spread[:, 0:P],
+                lhsT=v_of[b][:, 0:1].to_broadcast([P, P]),
+                rhs=identity[:],
+                start=True,
+                stop=True,
+            )
+            result = keep.tile([P, TOKENS], F32, name="result%d" % b)
+            for c in range(TILES_PER_BATCH):
+                cols = slice(c * P, (c + 1) * P)
+                nc.vector.scalar_tensor_tensor(
+                    out=result[:, cols],
+                    in0=kn_by_token[b][:, cols],
+                    scalar=u_of[b][:, c : c + 1],
+                    in1=spread[:, 0:P],
+                    op0=ALU.mult,
+                    op1=ALU.mult,
+                )
+            nc.sync.dma_start(
+                out=out[b].rearrange("(r c) e -> r (c e)", c=TILES_PER_BATCH), in_=result[:]
+            )

@@ -22,6 +22,8 @@ TOKEN_TILES = BATCH * TILES_PER_BATCH
 EPS = 1e-6
 ROUNDS = 8
 
+REPEAT = 64
+
 SLICE_D = 4096
 SLICES = D // SLICE_D
 SLICE_PASSES = SLICE_D // K_PASS
@@ -175,23 +177,23 @@ def tile_sinkhornrouter_k_kernel(tc, x, w_gate, out):
             bank = banks.tile([P, BANK_WORDS], F32, name="bank")
             for c in range(TILES_PER_BATCH):
                 nc.tensor.matmul(
-                    out=bank[:, c : c + 1],
+                    out=bank[:, c * REPEAT : (c + 1) * REPEAT],
                     lhsT=kn_by_expert[b][:, c * P : (c + 1) * P],
-                    rhs=v[:, 0:1],
+                    rhs=v[:, 0:1].to_broadcast([P, REPEAT]),
                     start=True,
                     stop=True,
                 )
             u = vectors.tile([P, TILES_PER_BATCH], F32, name="u%d" % b)
-            nc.vector.reciprocal(out=u[:], in_=bank[:, 0:TILES_PER_BATCH])
+            nc.vector.reciprocal(out=u[:], in_=bank[:, 0 : TILES_PER_BATCH * REPEAT : REPEAT])
             return u
 
         def token_step(b, u):
             bank = banks.tile([P, BANK_WORDS], F32, name="bank")
             for c in range(TILES_PER_BATCH):
                 nc.tensor.matmul(
-                    out=bank[:, 0:1],
+                    out=bank[:, 0:REPEAT],
                     lhsT=kn_by_token[b][:, c * P : (c + 1) * P],
-                    rhs=u[:, c : c + 1],
+                    rhs=u[:, c : c + 1].to_broadcast([P, REPEAT]),
                     start=(c == 0),
                     stop=(c == TILES_PER_BATCH - 1),
                 )

@@ -14,33 +14,45 @@ P = 128
 PACK = 4
 K_PASS = P * PACK
 HALVES = 2
+PASS_WORDS = HALVES * P
 BANK_WORDS = 512
+BANK_PASSES = BANK_WORDS // PASS_WORDS
 
 BATCH, TOKENS, D, EXPERTS = 2, 512, 16384, 128
 TILES_PER_BATCH = TOKENS // P
 TOKEN_TILES = BATCH * TILES_PER_BATCH
+PASSES = D // K_PASS
 EPS = 1e-6
 ROUNDS = 8
 
+LOAD_PASSES = 16
+SMALLEST_LOAD = 4
+UNIT_PASSES = 8
+VECTOR_EVERY = 4
+RUN = 2
+
 REPEAT = 64
 
-SLICE_D = 4096
-SLICES = D // SLICE_D
-SLICE_PASSES = SLICE_D // K_PASS
-BANK_PASSES = BANK_WORDS // (HALVES * P)
-SLICE_BANKS = SLICE_PASSES // BANK_PASSES
-SLICE_COLS = SLICE_PASSES * P
-
 FLOPS = 2 * BATCH * TOKENS * D * EXPERTS
+
+
+def halving_cuts(total, smallest):
+    cuts = []
+    left = total
+    while left > smallest:
+        cuts.append(left // 2)
+        left -= left // 2
+    cuts.append(left)
+    return cuts
 
 
 def tile_sinkhornrouter_k_kernel(tc, x, w_gate, out):
     nc = tc.nc
     with ExitStack() as stack:
         keep = stack.enter_context(tc.tile_pool(name="keep", bufs=1))
-        raw_pool = stack.enter_context(tc.tile_pool(name="raw", bufs=8))
+        raw_pool = stack.enter_context(tc.tile_pool(name="raw", bufs=6))
         grouped_pool = stack.enter_context(tc.tile_pool(name="grouped", bufs=3))
-        x_mx_pool = stack.enter_context(tc.tile_pool(name="x_mx", bufs=3))
+        x_mx_pool = stack.enter_context(tc.tile_pool(name="x_mx", bufs=4))
         vectors = stack.enter_context(tc.tile_pool(name="vectors", bufs=2))
         banks = stack.enter_context(tc.psum_pool(name="banks", bufs=6))
         gate_banks = stack.enter_context(tc.psum_pool(name="gate_banks", bufs=2))
@@ -51,8 +63,8 @@ def tile_sinkhornrouter_k_kernel(tc, x, w_gate, out):
         ones = keep.tile([P, 1], F32, name="ones")
         nc.vector.memset(ones[:], 1.0)
 
-        w_codes = keep.tile([P, D // K_PASS * EXPERTS], U32, name="w_codes", align_bytes=64)
-        w_scales = keep.tile([P, D // K_PASS * EXPERTS], U8, name="w_scales", align_bytes=64)
+        w_codes = keep.tile([P, PASSES * EXPERTS], U32, name="w_codes", align_bytes=64)
+        w_scales = keep.tile([P, PASSES * EXPERTS], U8, name="w_scales", align_bytes=64)
 
         k_by_expert = [keep.tile([P, TOKENS], F32, name="k_by_expert%d" % b) for b in range(BATCH)]
         tile_sums = [keep.tile([P, TILES_PER_BATCH], F32, name="tile_sums%d" % b) for b in range(BATCH)]
@@ -64,74 +76,95 @@ def tile_sinkhornrouter_k_kernel(tc, x, w_gate, out):
             for j in range(TOKEN_TILES)
         ]
 
-        slices = []
-        for s in range(SLICES):
-            slices.append((w_gate, None, s))
-            slices.append((token_rows[0], 0, s))
-        for j in range(1, TOKEN_TILES):
-            for s in range(SLICES):
-                slices.append((token_rows[j], j, s))
+        falling = halving_cuts(PASSES, SMALLEST_LOAD)
+        rising = list(reversed(falling))
+        loads = []
+        first = 0
+        for passes in rising:
+            loads.append((w_gate, None, first, passes))
+            loads.append((token_rows[0], 0, first, passes))
+            first += passes
+        for j in range(1, TOKEN_TILES - 1):
+            for first in range(0, PASSES, LOAD_PASSES):
+                loads.append((token_rows[j], j, first, LOAD_PASSES))
+        first = 0
+        for passes in falling:
+            loads.append((token_rows[TOKEN_TILES - 1], TOKEN_TILES - 1, first, passes))
+            first += passes
 
+        units = []
+        for n, (rows, j, first, passes) in enumerate(loads):
+            for inside in range(0, passes, UNIT_PASSES):
+                units.append((n, j, first + inside, min(UNIT_PASSES, passes - inside), inside))
+
+        raw_of = {}
         grouped_of = {}
         mx_of = {}
         gates_of = {}
 
-        def transpose_slice(i):
-            rows, j, s = slices[i]
-            raw = raw_pool.tile([P, SLICE_D], BF16, name="raw")
-            nc.sync.dma_start(out=raw[:], in_=rows[:, s * SLICE_D : (s + 1) * SLICE_D])
-            raw_words = raw[:].bitcast(F32)
-            grouped = grouped_pool.tile([P, SLICE_D], BF16, name="grouped", align_bytes=64)
+        def transpose_unit(i):
+            n, j, first, passes, inside = units[i]
+            if inside == 0:
+                rows, j, first, load_passes = loads[n]
+                raw = raw_pool.tile([P, LOAD_PASSES * K_PASS], BF16, name="raw")
+                nc.sync.dma_start(
+                    out=raw[:, 0 : load_passes * K_PASS],
+                    in_=rows[:, first * K_PASS : (first + load_passes) * K_PASS],
+                )
+                raw_of[n] = raw
+            raw_words = raw_of[n][:].bitcast(F32)
+            grouped = grouped_pool.tile([P, UNIT_PASSES * P * PACK], BF16, name="grouped", align_bytes=64)
             grouped_words = grouped[:].bitcast(F32).rearrange(
-                "p (g r u) -> p g r u", g=SLICE_PASSES, u=HALVES
+                "p (g r u) -> p g r u", g=UNIT_PASSES, u=HALVES
             )
-            for k in range(SLICE_BANKS):
+            for k in range(passes // BANK_PASSES):
                 bank = banks.tile([P, BANK_WORDS], F32, name="bank")
-                for t in range(BANK_PASSES * HALVES):
-                    first = (k * BANK_PASSES * HALVES + t) * P
+                for t in range(BANK_WORDS // P):
+                    word = (inside + k * BANK_PASSES) * PASS_WORDS + t * P
                     nc.tensor.transpose(
-                        bank[:, t * P : (t + 1) * P], raw_words[:, first : first + P], identity[:]
+                        bank[:, t * P : (t + 1) * P], raw_words[:, word : word + P], identity[:]
                     )
-                copy = nc.vector.tensor_copy if k == 0 else nc.scalar.copy
+                copy = nc.vector.tensor_copy if k % VECTOR_EVERY == 0 else nc.scalar.copy
                 copy(
                     out=grouped_words[:, k * BANK_PASSES : (k + 1) * BANK_PASSES, :, :],
                     in_=bank[:].rearrange("p (g u r) -> p g r u", g=BANK_PASSES, u=HALVES),
                 )
             grouped_of[i] = grouped
 
-        def quantise_slice(i):
-            rows, j, s = slices[i]
+        def quantise_unit(i):
+            n, j, first, passes, inside = units[i]
             if j is None:
-                cols = slice(s * SLICE_COLS, (s + 1) * SLICE_COLS)
+                cols = slice(first * P, (first + passes) * P)
                 codes, scales = w_codes[:, cols], w_scales[:, cols]
             else:
-                x_codes = x_mx_pool.tile([P, SLICE_COLS], U32, name="x_codes", align_bytes=64)
-                x_scales = x_mx_pool.tile([P, SLICE_COLS], U8, name="x_scales", align_bytes=64)
-                codes, scales = x_codes[:], x_scales[:]
+                x_codes = x_mx_pool.tile([P, UNIT_PASSES * P], U32, name="x_codes", align_bytes=64)
+                x_scales = x_mx_pool.tile([P, UNIT_PASSES * P], U8, name="x_scales", align_bytes=64)
+                codes, scales = x_codes[:, 0 : passes * P], x_scales[:, 0 : passes * P]
                 mx_of[i] = (codes, scales)
-            nc.vector.quantize_mx(out=codes.bitcast(FP8X4), scales=scales, in_=grouped_of[i][:])
+            nc.vector.quantize_mx(
+                out=codes.bitcast(FP8X4), scales=scales, in_=grouped_of[i][:, 0 : passes * P * PACK]
+            )
 
-        def multiply_slice(i):
-            rows, j, s = slices[i]
+        def multiply_unit(i):
+            n, j, first, passes, inside = units[i]
             if j is None:
                 return
-            if s == 0:
+            if first == 0:
                 gates_of[j] = gate_banks.tile([P, P], F32, name="gates")
-            gates = gates_of[j]
             codes, scales = mx_of[i]
-            for g in range(SLICE_PASSES):
-                w_cols = slice((s * SLICE_PASSES + g) * P, (s * SLICE_PASSES + g + 1) * P)
+            for g in range(passes):
+                w_cols = slice((first + g) * P, (first + g + 1) * P)
                 x_cols = slice(g * P, (g + 1) * P)
                 nc.tensor.matmul_mx(
-                    out=gates[:],
+                    out=gates_of[j][:],
                     lhsT=w_codes[:, w_cols].bitcast(FP8X4),
                     lhsT_scale=w_scales[:, w_cols],
                     rhs=codes[:, x_cols].bitcast(FP8X4),
                     rhs_scale=scales[:, x_cols],
-                    start=(s == 0 and g == 0),
-                    stop=(s == SLICES - 1 and g == SLICE_PASSES - 1),
+                    start=(first + g == 0),
+                    stop=(first + g == PASSES - 1),
                 )
-            if s == SLICES - 1:
+            if first + passes == PASSES:
                 clamp_tile(j)
 
         def clamp_tile(j):
@@ -158,13 +191,16 @@ def tile_sinkhornrouter_k_kernel(tc, x, w_gate, out):
                     op0=ALU.mult,
                 )
 
-        for i in range(len(slices) + 2):
-            if i < len(slices):
-                transpose_slice(i)
-            if 0 <= i - 1 < len(slices):
-                quantise_slice(i - 1)
-            if 0 <= i - 2:
-                multiply_slice(i - 2)
+        multiplied = 0
+        for i in range(len(units) + 2):
+            if i < len(units):
+                transpose_unit(i)
+            if 0 <= i - 1 < len(units):
+                quantise_unit(i - 1)
+            if i % RUN == RUN - 1 or i >= len(units):
+                for m in range(multiplied, i - 1):
+                    multiply_unit(m)
+                multiplied = max(multiplied, i - 1)
 
         for b in range(BATCH):
             bank = banks.tile([P, BANK_WORDS], F32, name="bank")
@@ -202,34 +238,31 @@ def tile_sinkhornrouter_k_kernel(tc, x, w_gate, out):
             return v
 
         v_of = [ones, ones]
-        u_of = [None, None]
-        for r in range(ROUNDS):
-            if r > 0:
-                for b in range(BATCH):
-                    v_of[b] = token_step(b, u_of[b])
-            for b in range(BATCH):
-                u_of[b] = expert_step(b, v_of[b])
+        for r in range(ROUNDS - 1):
+            u_of = [expert_step(b, v_of[b]) for b in range(BATCH)]
+            v_of = [token_step(b, u_of[b]) for b in range(BATCH)]
+
+        def by_tile(ap):
+            return ap.rearrange("p (c e) -> p c e", c=TILES_PER_BATCH)
 
         for b in range(BATCH):
             spread = banks.tile([P, BANK_WORDS], F32, name="bank")
-            nc.tensor.matmul(
-                out=spread[:, 0:P],
-                lhsT=v_of[b][:, 0:1].to_broadcast([P, P]),
-                rhs=identity[:],
-                start=True,
-                stop=True,
+            nc.tensor.transpose(spread[:, 0:P], v_of[b][:, 0:1].to_broadcast([P, P]), identity[:])
+            scaled = keep.tile([P, TOKENS], F32, name="scaled%d" % b)
+            nc.vector.tensor_tensor(
+                out=by_tile(scaled[:]),
+                in0=by_tile(kn_by_token[b][:]),
+                in1=spread[:, 0:P].unsqueeze(1).to_broadcast([P, TILES_PER_BATCH, P]),
+                op=ALU.mult,
             )
+            u = expert_step(b, v_of[b])
             result = keep.tile([P, TOKENS], F32, name="result%d" % b)
-            for c in range(TILES_PER_BATCH):
-                cols = slice(c * P, (c + 1) * P)
-                nc.vector.scalar_tensor_tensor(
-                    out=result[:, cols],
-                    in0=kn_by_token[b][:, cols],
-                    scalar=u_of[b][:, c : c + 1],
-                    in1=spread[:, 0:P],
-                    op0=ALU.mult,
-                    op1=ALU.mult,
-                )
+            nc.vector.tensor_tensor(
+                out=by_tile(result[:]),
+                in0=by_tile(scaled[:]),
+                in1=u[:].unsqueeze(2).to_broadcast([P, TILES_PER_BATCH, P]),
+                op=ALU.mult,
+            )
             nc.sync.dma_start(
                 out=out[b].rearrange("(r c) e -> r (c e)", c=TILES_PER_BATCH), in_=result[:]
             )

@@ -31,7 +31,7 @@ UNIT_PASSES = 8
 VECTOR_EVERY = 4
 RUN = 2
 
-REPEAT = 64
+REPEAT = 32
 
 FLOPS = 2 * BATCH * TOKENS * D * EXPERTS
 
@@ -67,9 +67,12 @@ def tile_sinkhornrouter_k_kernel(tc, x, w_gate, out):
         w_scales = keep.tile([P, PASSES * EXPERTS], U8, name="w_scales", align_bytes=64)
 
         k_by_expert = [keep.tile([P, TOKENS], F32, name="k_by_expert%d" % b) for b in range(BATCH)]
+        k_by_token = [keep.tile([P, TOKENS], F32, name="k_by_token%d" % b) for b in range(BATCH)]
         tile_sums = [keep.tile([P, TILES_PER_BATCH], F32, name="tile_sums%d" % b) for b in range(BATCH)]
-        kn_by_expert = [keep.tile([P, TOKENS], F32, name="kn_by_expert%d" % b) for b in range(BATCH)]
-        kn_by_token = [keep.tile([P, TOKENS], F32, name="kn_by_token%d" % b) for b in range(BATCH)]
+        hi_by_expert = [keep.tile([P, TOKENS], BF16, name="hi_by_expert%d" % b) for b in range(BATCH)]
+        lo_by_expert = [keep.tile([P, TOKENS], BF16, name="lo_by_expert%d" % b) for b in range(BATCH)]
+        hi_by_token = [keep.tile([P, TOKENS], BF16, name="hi_by_token%d" % b) for b in range(BATCH)]
+        lo_by_token = [keep.tile([P, TOKENS], BF16, name="lo_by_token%d" % b) for b in range(BATCH)]
 
         token_rows = [
             x[j // TILES_PER_BATCH].rearrange("(r c) d -> c r d", c=TILES_PER_BATCH)[j % TILES_PER_BATCH]
@@ -165,36 +168,51 @@ def tile_sinkhornrouter_k_kernel(tc, x, w_gate, out):
                     stop=(first + g == PASSES - 1),
                 )
             if first + passes == PASSES:
-                clamp_tile(j)
+                chores.extend(tile_chores(j))
 
-        def clamp_tile(j):
+        def tile_chores(j):
             b, c = divmod(j, TILES_PER_BATCH)
-            nc.vector.tensor_scalar(
-                out=k_by_expert[b][:, c * P : (c + 1) * P],
-                in0=gates_of[j][:],
-                scalar1=EPS,
-                scalar2=None,
-                op0=ALU.max,
-                op1=ALU.add,
-                accum_out=tile_sums[b][:, c : c + 1],
-            )
-            if c == TILES_PER_BATCH - 1:
-                column_sum = vectors.tile([P, 1], F32, name="column_sum")
-                nc.vector.reduce_sum(out=column_sum[:], in_=tile_sums[b][:], axis=mybir.AxisListType.X)
-                first_v = vectors.tile([P, 1], F32, name="first_v")
-                nc.vector.reciprocal(out=first_v[:], in_=column_sum[:])
+            cols = slice(c * P, (c + 1) * P)
+            turned = {}
+
+            def clamp():
                 nc.vector.tensor_scalar(
-                    out=kn_by_expert[b][:],
-                    in0=k_by_expert[b][:],
-                    scalar1=first_v[:, 0:1],
+                    out=k_by_expert[b][:, cols],
+                    in0=gates_of[j][:],
+                    scalar1=EPS,
                     scalar2=None,
-                    op0=ALU.mult,
+                    op0=ALU.max,
+                    op1=ALU.add,
+                    accum_out=tile_sums[b][:, c : c + 1],
                 )
 
+            def turn():
+                nc.scalar.copy(out=hi_by_expert[b][:, cols], in_=k_by_expert[b][:, cols])
+                bank = banks.tile([P, BANK_WORDS], F32, name="bank")
+                nc.tensor.transpose(bank[:, 0:P], k_by_expert[b][:, cols], identity[:])
+                nc.scalar.copy(out=hi_by_token[b][:, cols], in_=bank[:, 0:P])
+                nc.scalar.copy(out=k_by_token[b][:, cols], in_=bank[:, 0:P])
+
+            def split():
+                for lo, whole, hi in (
+                    (lo_by_expert, k_by_expert, hi_by_expert),
+                    (lo_by_token, k_by_token, hi_by_token),
+                ):
+                    nc.vector.tensor_tensor(
+                        out=lo[b][:, cols], in0=whole[b][:, cols], in1=hi[b][:, cols], op=ALU.subtract
+                    )
+
+            return [clamp, turn, split]
+
+        chores = []
+        done = 0
         multiplied = 0
         for i in range(len(units) + 2):
             if i < len(units):
                 transpose_unit(i)
+            if done < len(chores):
+                chores[done]()
+                done += 1
             if 0 <= i - 1 < len(units):
                 quantise_unit(i - 1)
             if i % RUN == RUN - 1 or i >= len(units):
@@ -202,42 +220,63 @@ def tile_sinkhornrouter_k_kernel(tc, x, w_gate, out):
                     multiply_unit(m)
                 multiplied = max(multiplied, i - 1)
 
-        for b in range(BATCH):
+        def pair_of_reciprocal(sums, width, name):
+            hi = vectors.tile([P, width], BF16, name=name + "_hi")
+            with nc.allow_low_precision(reason="hi is the first half of a pair; lo holds what it leaves out"):
+                nc.vector.reciprocal(out=hi[:], in_=sums)
+            whole = vectors.tile([P, width], F32, name=name + "_whole")
+            nc.vector.reciprocal(out=whole[:], in_=sums)
+            lo = vectors.tile([P, width], BF16, name=name + "_lo")
+            nc.vector.tensor_tensor(out=lo[:], in0=whole[:], in1=hi[:], op=ALU.subtract)
+            return whole, hi, lo
+
+        def first_token_step(b):
+            column_sum = vectors.tile([P, 1], F32, name="column_sum%d" % b)
+            nc.vector.reduce_sum(out=column_sum[:], in_=tile_sums[b][:], axis=mybir.AxisListType.X)
+            return pair_of_reciprocal(column_sum[:], 1, "v%d" % b)
+
+        def expert_step(b, v):
+            v_whole, v_hi, v_lo = v
             bank = banks.tile([P, BANK_WORDS], F32, name="bank")
             for c in range(TILES_PER_BATCH):
                 cols = slice(c * P, (c + 1) * P)
-                nc.tensor.transpose(bank[:, cols], kn_by_expert[b][:, cols], identity[:])
-            nc.scalar.copy(out=kn_by_token[b][:], in_=bank[:])
-
-        def expert_step(b, v):
-            bank = banks.tile([P, BANK_WORDS], F32, name="bank")
-            for c in range(TILES_PER_BATCH):
-                nc.tensor.matmul(
-                    out=bank[:, c * REPEAT : (c + 1) * REPEAT],
-                    lhsT=kn_by_expert[b][:, c * P : (c + 1) * P],
-                    rhs=v[:, 0:1].to_broadcast([P, REPEAT]),
-                    start=True,
-                    stop=True,
-                )
-            u = vectors.tile([P, TILES_PER_BATCH], F32, name="u%d" % b)
-            nc.vector.reciprocal(out=u[:], in_=bank[:, 0 : TILES_PER_BATCH * REPEAT : REPEAT])
-            return u
+                terms = [(hi_by_expert, v_hi), (lo_by_expert, v_hi), (hi_by_expert, v_lo)]
+                for t in range(len(terms)):
+                    matrix, vector = terms[t]
+                    nc.tensor.matmul(
+                        out=bank[:, c * REPEAT : (c + 1) * REPEAT],
+                        lhsT=matrix[b][:, cols],
+                        rhs=vector[:, 0:1].to_broadcast([P, REPEAT]),
+                        start=(t == 0),
+                        stop=(t == len(terms) - 1),
+                    )
+            return pair_of_reciprocal(
+                bank[:, 0 : TILES_PER_BATCH * REPEAT : REPEAT], TILES_PER_BATCH, "u%d" % b
+            )
 
         def token_step(b, u):
+            u_whole, u_hi, u_lo = u
             bank = banks.tile([P, BANK_WORDS], F32, name="bank")
-            for c in range(TILES_PER_BATCH):
+            terms = []
+            for matrix, vector in ((hi_by_token, u_hi), (lo_by_token, u_hi), (hi_by_token, u_lo)):
+                for c in range(TILES_PER_BATCH):
+                    terms.append((matrix, vector, c))
+            for t in range(len(terms)):
+                matrix, vector, c = terms[t]
                 nc.tensor.matmul(
                     out=bank[:, 0:REPEAT],
-                    lhsT=kn_by_token[b][:, c * P : (c + 1) * P],
-                    rhs=u[:, c : c + 1].to_broadcast([P, REPEAT]),
-                    start=(c == 0),
-                    stop=(c == TILES_PER_BATCH - 1),
+                    lhsT=matrix[b][:, c * P : (c + 1) * P],
+                    rhs=vector[:, c : c + 1].to_broadcast([P, REPEAT]),
+                    start=(t == 0),
+                    stop=(t == len(terms) - 1),
                 )
-            v = vectors.tile([P, 1], F32, name="v%d" % b)
-            nc.vector.reciprocal(out=v[:], in_=bank[:, 0:1])
-            return v
+            return pair_of_reciprocal(bank[:, 0:1], 1, "v%d" % b)
 
-        v_of = [ones, ones]
+        clamp, turn, split = chores[done:]
+        clamp()
+        v_of = [first_token_step(b) for b in range(BATCH)]
+        turn()
+        split()
         for r in range(ROUNDS - 1):
             u_of = [expert_step(b, v_of[b]) for b in range(BATCH)]
             v_of = [token_step(b, u_of[b]) for b in range(BATCH)]
@@ -246,21 +285,22 @@ def tile_sinkhornrouter_k_kernel(tc, x, w_gate, out):
             return ap.rearrange("p (c e) -> p c e", c=TILES_PER_BATCH)
 
         for b in range(BATCH):
+            v_whole, v_hi, v_lo = v_of[b]
             spread = banks.tile([P, BANK_WORDS], F32, name="bank")
-            nc.tensor.transpose(spread[:, 0:P], v_of[b][:, 0:1].to_broadcast([P, P]), identity[:])
+            nc.tensor.transpose(spread[:, 0:P], v_whole[:, 0:1].to_broadcast([P, P]), identity[:])
             scaled = keep.tile([P, TOKENS], F32, name="scaled%d" % b)
             nc.vector.tensor_tensor(
                 out=by_tile(scaled[:]),
-                in0=by_tile(kn_by_token[b][:]),
+                in0=by_tile(k_by_token[b][:]),
                 in1=spread[:, 0:P].unsqueeze(1).to_broadcast([P, TILES_PER_BATCH, P]),
                 op=ALU.mult,
             )
-            u = expert_step(b, v_of[b])
+            u_whole, u_hi, u_lo = expert_step(b, v_of[b])
             result = keep.tile([P, TOKENS], F32, name="result%d" % b)
             nc.vector.tensor_tensor(
                 out=by_tile(result[:]),
                 in0=by_tile(scaled[:]),
-                in1=u[:].unsqueeze(2).to_broadcast([P, TILES_PER_BATCH, P]),
+                in1=u_whole[:].unsqueeze(2).to_broadcast([P, TILES_PER_BATCH, P]),
                 op=ALU.mult,
             )
             nc.sync.dma_start(

@@ -26,8 +26,9 @@ EPS = 1e-6
 ROUNDS = 8
 
 LOAD_PASSES = 16
-SMALLEST_LOAD = 4
 UNIT_PASSES = 8
+SMALLEST_FIRST_LOAD = 4
+SMALLEST_LAST_LOAD = 2
 VECTOR_EVERY = 4
 RUN = 2
 
@@ -79,8 +80,8 @@ def tile_sinkhornrouter_k_kernel(tc, x, w_gate, out):
             for j in range(TOKEN_TILES)
         ]
 
-        falling = halving_cuts(PASSES, SMALLEST_LOAD)
-        rising = list(reversed(falling))
+        rising = list(reversed(halving_cuts(PASSES, SMALLEST_FIRST_LOAD)))
+        falling = [UNIT_PASSES] * (PASSES // UNIT_PASSES - 1) + halving_cuts(UNIT_PASSES, SMALLEST_LAST_LOAD)
         loads = []
         first = 0
         for passes in rising:

@@ -14,37 +14,33 @@ P = 128
 PACK = 4
 K_PASS = P * PACK
 HALVES = 2
-PASS_WORDS = HALVES * P
 BANK_WORDS = 512
-BANK_PASSES = BANK_WORDS // PASS_WORDS
+BANK_PIECES = BANK_WORDS // (HALVES * P)
 
 BATCH, TOKENS, D, EXPERTS = 2, 512, 16384, 128
 TILES_PER_BATCH = TOKENS // P
-TOKEN_TILES = BATCH * TILES_PER_BATCH
+GROUP_TILES = 1
+GROUP = GROUP_TILES * P
+GROUPS_PER_BATCH = TILES_PER_BATCH // GROUP_TILES
+GROUPS = BATCH * GROUPS_PER_BATCH
 PASSES = D // K_PASS
 EPS = 1e-6
 ROUNDS = 8
 
-LOAD_PASSES = 16
-UNIT_PASSES = 8
+UNIT_PIECES = 8
+LOAD_PIECES = 16
+SMALL_LOAD_PIECES = 8
+SMALL_LOAD_GROUPS = 3
 SMALLEST_FIRST_LOAD = 4
 SMALLEST_LAST_LOAD = 2
-VECTOR_EVERY = 4
+VECTOR_BANK, BANKS_IN_TURN = 1, 4
 RUN = 2
+LAST_UNITS = 4
+EARLY_STEPS = 4
 
 REPEAT = 32
 
 FLOPS = 2 * BATCH * TOKENS * D * EXPERTS
-
-
-def halving_cuts(total, smallest):
-    cuts = []
-    left = total
-    while left > smallest:
-        cuts.append(left // 2)
-        left -= left // 2
-    cuts.append(left)
-    return cuts
 
 
 def tile_sinkhornrouter_k_kernel(tc, x, w_gate, out):
@@ -53,53 +49,67 @@ def tile_sinkhornrouter_k_kernel(tc, x, w_gate, out):
         keep = stack.enter_context(tc.tile_pool(name="keep", bufs=1))
         raw_pool = stack.enter_context(tc.tile_pool(name="raw", bufs=6))
         grouped_pool = stack.enter_context(tc.tile_pool(name="grouped", bufs=3))
-        x_mx_pool = stack.enter_context(tc.tile_pool(name="x_mx", bufs=4))
+        x_mx_pool = stack.enter_context(tc.tile_pool(name="x_mx", bufs=8))
         vectors = stack.enter_context(tc.tile_pool(name="vectors", bufs=2))
-        banks = stack.enter_context(tc.psum_pool(name="banks", bufs=6))
+        banks = stack.enter_context(tc.psum_pool(name="banks", bufs=5))
         gate_banks = stack.enter_context(tc.psum_pool(name="gate_banks", bufs=2))
+        early_banks = stack.enter_context(tc.psum_pool(name="early_banks", bufs=1))
         stack.enter_context(tc.manual_schedule())
 
         identity = keep.tile([P, P], F32, name="identity")
         make_identity(nc, identity[:])
-        ones = keep.tile([P, 1], F32, name="ones")
-        nc.vector.memset(ones[:], 1.0)
 
         w_codes = keep.tile([P, PASSES * EXPERTS], U32, name="w_codes", align_bytes=64)
         w_scales = keep.tile([P, PASSES * EXPERTS], U8, name="w_scales", align_bytes=64)
 
         k_by_expert = [keep.tile([P, TOKENS], F32, name="k_by_expert%d" % b) for b in range(BATCH)]
         k_by_token = [keep.tile([P, TOKENS], F32, name="k_by_token%d" % b) for b in range(BATCH)]
-        tile_sums = [keep.tile([P, TILES_PER_BATCH], F32, name="tile_sums%d" % b) for b in range(BATCH)]
+        group_sums = [keep.tile([P, GROUPS_PER_BATCH], F32, name="group_sums%d" % b) for b in range(BATCH)]
         hi_by_expert = [keep.tile([P, TOKENS], BF16, name="hi_by_expert%d" % b) for b in range(BATCH)]
         lo_by_expert = [keep.tile([P, TOKENS], BF16, name="lo_by_expert%d" % b) for b in range(BATCH)]
         hi_by_token = [keep.tile([P, TOKENS], BF16, name="hi_by_token%d" % b) for b in range(BATCH)]
         lo_by_token = [keep.tile([P, TOKENS], BF16, name="lo_by_token%d" % b) for b in range(BATCH)]
 
-        token_rows = [
-            x[j // TILES_PER_BATCH].rearrange("(r c) d -> c r d", c=TILES_PER_BATCH)[j % TILES_PER_BATCH]
-            for j in range(TOKEN_TILES)
-        ]
+        w_rows = w_gate.rearrange("(r c) d -> r c d", c=1)
+        group_rows = []
+        for b in range(BATCH):
+            by_row = x[b].rearrange("(r c) d -> r c d", c=TILES_PER_BATCH)
+            for c in range(0, TILES_PER_BATCH, GROUP_TILES):
+                group_rows.append(by_row[:, c : c + GROUP_TILES, :])
 
-        rising = list(reversed(halving_cuts(PASSES, SMALLEST_FIRST_LOAD)))
-        falling = [UNIT_PASSES] * (PASSES // UNIT_PASSES - 1) + halving_cuts(UNIT_PASSES, SMALLEST_LAST_LOAD)
+        def cuts(total, most, smallest):
+            sizes = []
+            left = total
+            while left > most:
+                sizes.append(most)
+                left -= most
+            while left > smallest:
+                sizes.append(left // 2)
+                left -= left // 2
+            sizes.append(left)
+            return sizes
+
         loads = []
-        first = 0
-        for passes in rising:
-            loads.append((w_gate, None, first, passes))
-            loads.append((token_rows[0], 0, first, passes))
-            first += passes
-        for j in range(1, TOKEN_TILES - 1):
-            for first in range(0, PASSES, LOAD_PASSES):
-                loads.append((token_rows[j], j, first, LOAD_PASSES))
-        first = 0
-        for passes in falling:
-            loads.append((token_rows[TOKEN_TILES - 1], TOKEN_TILES - 1, first, passes))
-            first += passes
+        for j in range(GROUPS):
+            most = LOAD_PIECES if j < GROUPS - SMALL_LOAD_GROUPS else SMALL_LOAD_PIECES
+            sizes = cuts(PASSES, most // GROUP_TILES, PASSES)
+            if j == 0:
+                sizes = list(reversed(cuts(PASSES, most // GROUP_TILES, SMALLEST_FIRST_LOAD)))
+            if j == GROUPS - 1:
+                sizes = cuts(PASSES, most // GROUP_TILES, SMALLEST_LAST_LOAD // GROUP_TILES)
+            first = 0
+            for passes in sizes:
+                if j == 0:
+                    loads.append((w_rows, 1, None, first, passes))
+                loads.append((group_rows[j], GROUP_TILES, j, first, passes))
+                first += passes
 
         units = []
-        for n, (rows, j, first, passes) in enumerate(loads):
-            for inside in range(0, passes, UNIT_PASSES):
-                units.append((n, j, first + inside, min(UNIT_PASSES, passes - inside), inside))
+        for n in range(len(loads)):
+            rows, tiles, j, first, passes = loads[n]
+            step = UNIT_PIECES // tiles
+            for inside in range(0, passes, step):
+                units.append((n, tiles, j, first + inside, min(step, passes - inside), inside))
 
         raw_of = {}
         grouped_of = {}
@@ -107,60 +117,60 @@ def tile_sinkhornrouter_k_kernel(tc, x, w_gate, out):
         gates_of = {}
 
         def transpose_unit(i):
-            n, j, first, passes, inside = units[i]
+            n, tiles, j, first, passes, inside = units[i]
+            rows, tiles, j, load_first, load_passes = loads[n]
             if inside == 0:
-                rows, j, first, load_passes = loads[n]
-                raw = raw_pool.tile([P, LOAD_PASSES * K_PASS], BF16, name="raw")
+                raw = raw_pool.tile([P, LOAD_PIECES * K_PASS], BF16, name="raw")
                 nc.sync.dma_start(
-                    out=raw[:, 0 : load_passes * K_PASS],
-                    in_=rows[:, first * K_PASS : (first + load_passes) * K_PASS],
+                    out=raw[:, 0 : tiles * load_passes * K_PASS].rearrange("p (c d) -> p c d", c=tiles),
+                    in_=rows[:, :, load_first * K_PASS : (load_first + load_passes) * K_PASS],
                 )
                 raw_of[n] = raw
             raw_words = raw_of[n][:].bitcast(F32)
-            grouped = grouped_pool.tile([P, UNIT_PASSES * P * PACK], BF16, name="grouped", align_bytes=64)
-            grouped_words = grouped[:].bitcast(F32).rearrange(
-                "p (g r u) -> p g r u", g=UNIT_PASSES, u=HALVES
-            )
-            for k in range(passes // BANK_PASSES):
+            grouped = grouped_pool.tile([P, UNIT_PIECES * P * PACK], BF16, name="grouped", align_bytes=64)
+            grouped_words = grouped[:].bitcast(F32).rearrange("p (s r u) -> p s r u", s=UNIT_PIECES, u=HALVES)
+            for k in range(passes * tiles // BANK_PIECES):
                 bank = banks.tile([P, BANK_WORDS], F32, name="bank")
-                for t in range(BANK_WORDS // P):
-                    word = (inside + k * BANK_PASSES) * PASS_WORDS + t * P
-                    nc.tensor.transpose(
-                        bank[:, t * P : (t + 1) * P], raw_words[:, word : word + P], identity[:]
-                    )
-                copy = nc.vector.tensor_copy if k % VECTOR_EVERY == 0 else nc.scalar.copy
+                for t in range(BANK_PIECES):
+                    g, c = divmod(k * BANK_PIECES + t, tiles)
+                    for u in range(HALVES):
+                        word = ((c * load_passes + inside + g) * HALVES + u) * P
+                        at = (t * HALVES + u) * P
+                        nc.tensor.transpose(bank[:, at : at + P], raw_words[:, word : word + P], identity[:])
+                copy = nc.vector.tensor_copy if k % BANKS_IN_TURN == VECTOR_BANK else nc.scalar.copy
                 copy(
-                    out=grouped_words[:, k * BANK_PASSES : (k + 1) * BANK_PASSES, :, :],
-                    in_=bank[:].rearrange("p (g u r) -> p g r u", g=BANK_PASSES, u=HALVES),
+                    out=grouped_words[:, k * BANK_PIECES : (k + 1) * BANK_PIECES, :, :],
+                    in_=bank[:].rearrange("p (s u r) -> p s r u", s=BANK_PIECES, u=HALVES),
                 )
             grouped_of[i] = grouped
 
         def quantise_unit(i):
-            n, j, first, passes, inside = units[i]
+            n, tiles, j, first, passes, inside = units[i]
+            columns = passes * tiles * P
             if j is None:
                 cols = slice(first * P, (first + passes) * P)
                 codes, scales = w_codes[:, cols], w_scales[:, cols]
             else:
-                x_codes = x_mx_pool.tile([P, UNIT_PASSES * P], U32, name="x_codes", align_bytes=64)
-                x_scales = x_mx_pool.tile([P, UNIT_PASSES * P], U8, name="x_scales", align_bytes=64)
-                codes, scales = x_codes[:, 0 : passes * P], x_scales[:, 0 : passes * P]
+                x_codes = x_mx_pool.tile([P, UNIT_PIECES * P], U32, name="x_codes", align_bytes=64)
+                x_scales = x_mx_pool.tile([P, UNIT_PIECES * P], U8, name="x_scales", align_bytes=64)
+                codes, scales = x_codes[:, 0:columns], x_scales[:, 0:columns]
                 mx_of[i] = (codes, scales)
             nc.vector.quantize_mx(
-                out=codes.bitcast(FP8X4), scales=scales, in_=grouped_of[i][:, 0 : passes * P * PACK]
+                out=codes.bitcast(FP8X4), scales=scales, in_=grouped_of[i][:, 0 : columns * PACK]
             )
 
         def multiply_unit(i):
-            n, j, first, passes, inside = units[i]
+            n, tiles, j, first, passes, inside = units[i]
             if j is None:
                 return
             if first == 0:
-                gates_of[j] = gate_banks.tile([P, P], F32, name="gates")
+                gates_of[j] = gate_banks.tile([P, BANK_WORDS], F32, name="gates")
             codes, scales = mx_of[i]
             for g in range(passes):
                 w_cols = slice((first + g) * P, (first + g + 1) * P)
-                x_cols = slice(g * P, (g + 1) * P)
+                x_cols = slice(g * GROUP, (g + 1) * GROUP)
                 nc.tensor.matmul_mx(
-                    out=gates_of[j][:],
+                    out=gates_of[j][:, 0:GROUP],
                     lhsT=w_codes[:, w_cols].bitcast(FP8X4),
                     lhsT_scale=w_scales[:, w_cols],
                     rhs=codes[:, x_cols].bitcast(FP8X4),
@@ -169,30 +179,33 @@ def tile_sinkhornrouter_k_kernel(tc, x, w_gate, out):
                     stop=(first + g == PASSES - 1),
                 )
             if first + passes == PASSES:
-                chores.extend(tile_chores(j))
+                chores.extend(group_chores(j))
 
-        def tile_chores(j):
-            b, c = divmod(j, TILES_PER_BATCH)
-            cols = slice(c * P, (c + 1) * P)
-            turned = {}
+        def group_chores(j):
+            b, q = divmod(j, GROUPS_PER_BATCH)
+            cols = slice(q * GROUP, (q + 1) * GROUP)
 
             def clamp():
                 nc.vector.tensor_scalar(
                     out=k_by_expert[b][:, cols],
-                    in0=gates_of[j][:],
+                    in0=gates_of[j][:, 0:GROUP],
                     scalar1=EPS,
                     scalar2=None,
                     op0=ALU.max,
                     op1=ALU.add,
-                    accum_out=tile_sums[b][:, c : c + 1],
+                    accum_out=group_sums[b][:, q : q + 1],
                 )
 
             def turn():
                 nc.scalar.copy(out=hi_by_expert[b][:, cols], in_=k_by_expert[b][:, cols])
                 bank = banks.tile([P, BANK_WORDS], F32, name="bank")
-                nc.tensor.transpose(bank[:, 0:P], k_by_expert[b][:, cols], identity[:])
-                nc.scalar.copy(out=hi_by_token[b][:, cols], in_=bank[:, 0:P])
-                nc.scalar.copy(out=k_by_token[b][:, cols], in_=bank[:, 0:P])
+                for c in range(GROUP_TILES):
+                    at = q * GROUP + c * P
+                    nc.tensor.transpose(
+                        bank[:, c * P : (c + 1) * P], k_by_expert[b][:, at : at + P], identity[:]
+                    )
+                nc.scalar.copy(out=hi_by_token[b][:, cols], in_=bank[:, 0:GROUP])
+                nc.scalar.copy(out=k_by_token[b][:, cols], in_=bank[:, 0:GROUP])
 
             def split():
                 for lo, whole, hi in (
@@ -205,105 +218,152 @@ def tile_sinkhornrouter_k_kernel(tc, x, w_gate, out):
 
             return [clamp, turn, split]
 
-        chores = []
-        done = 0
-        multiplied = 0
-        for i in range(len(units) + 2):
-            if i < len(units):
-                transpose_unit(i)
-            if done < len(chores):
-                chores[done]()
-                done += 1
-            if 0 <= i - 1 < len(units):
-                quantise_unit(i - 1)
-            if i % RUN == RUN - 1 or i >= len(units):
-                for m in range(multiplied, i - 1):
-                    multiply_unit(m)
-                multiplied = max(multiplied, i - 1)
-
         def pair_of_reciprocal(sums, width, name):
-            hi = vectors.tile([P, width], BF16, name=name + "_hi")
-            with nc.allow_low_precision(reason="hi is the first half of a pair; lo holds what it leaves out"):
-                nc.vector.reciprocal(out=hi[:], in_=sums)
             whole = vectors.tile([P, width], F32, name=name + "_whole")
             nc.vector.reciprocal(out=whole[:], in_=sums)
+            hi = whole[:].bitcast(BF16)[:, 1 : 2 * width : 2]
             lo = vectors.tile([P, width], BF16, name=name + "_lo")
-            nc.vector.tensor_tensor(out=lo[:], in0=whole[:], in1=hi[:], op=ALU.subtract)
-            return whole, hi, lo
-
-        def first_token_step(b):
-            column_sum = vectors.tile([P, 1], F32, name="column_sum%d" % b)
-            nc.vector.reduce_sum(out=column_sum[:], in_=tile_sums[b][:], axis=mybir.AxisListType.X)
-            return pair_of_reciprocal(column_sum[:], 1, "v%d" % b)
-
-        def expert_step(b, v):
-            v_whole, v_hi, v_lo = v
-            bank = banks.tile([P, BANK_WORDS], F32, name="bank")
-            for c in range(TILES_PER_BATCH):
-                cols = slice(c * P, (c + 1) * P)
-                terms = [(hi_by_expert, v_hi), (lo_by_expert, v_hi), (hi_by_expert, v_lo)]
-                for t in range(len(terms)):
-                    matrix, vector = terms[t]
-                    nc.tensor.matmul(
-                        out=bank[:, c * REPEAT : (c + 1) * REPEAT],
-                        lhsT=matrix[b][:, cols],
-                        rhs=vector[:, 0:1].to_broadcast([P, REPEAT]),
-                        start=(t == 0),
-                        stop=(t == len(terms) - 1),
-                    )
-            return pair_of_reciprocal(
-                bank[:, 0 : TILES_PER_BATCH * REPEAT : REPEAT], TILES_PER_BATCH, "u%d" % b
-            )
-
-        def token_step(b, u):
-            u_whole, u_hi, u_lo = u
-            bank = banks.tile([P, BANK_WORDS], F32, name="bank")
-            terms = []
-            for matrix, vector in ((hi_by_token, u_hi), (lo_by_token, u_hi), (hi_by_token, u_lo)):
-                for c in range(TILES_PER_BATCH):
-                    terms.append((matrix, vector, c))
-            for t in range(len(terms)):
-                matrix, vector, c = terms[t]
-                nc.tensor.matmul(
-                    out=bank[:, 0:REPEAT],
-                    lhsT=matrix[b][:, c * P : (c + 1) * P],
-                    rhs=vector[:, c : c + 1].to_broadcast([P, REPEAT]),
-                    start=(t == 0),
-                    stop=(t == len(terms) - 1),
-                )
-            return pair_of_reciprocal(bank[:, 0:1], 1, "v%d" % b)
-
-        clamp, turn, split = chores[done:]
-        clamp()
-        v_of = [first_token_step(b) for b in range(BATCH)]
-        turn()
-        split()
-        for r in range(ROUNDS - 1):
-            u_of = [expert_step(b, v_of[b]) for b in range(BATCH)]
-            v_of = [token_step(b, u_of[b]) for b in range(BATCH)]
+            nc.vector.tensor_tensor(out=lo[:], in0=whole[:], in1=hi, op=ALU.subtract)
+            return whole, hi, lo[:]
 
         def by_tile(ap):
             return ap.rearrange("p (c e) -> p c e", c=TILES_PER_BATCH)
 
-        for b in range(BATCH):
-            v_whole, v_hi, v_lo = v_of[b]
-            spread = banks.tile([P, BANK_WORDS], F32, name="bank")
-            nc.tensor.transpose(spread[:, 0:P], v_whole[:, 0:1].to_broadcast([P, P]), identity[:])
-            scaled = keep.tile([P, TOKENS], F32, name="scaled%d" % b)
-            nc.vector.tensor_tensor(
-                out=by_tile(scaled[:]),
-                in0=by_tile(k_by_token[b][:]),
-                in1=spread[:, 0:P].unsqueeze(1).to_broadcast([P, TILES_PER_BATCH, P]),
-                op=ALU.mult,
-            )
-            u_whole, u_hi, u_lo = expert_step(b, v_of[b])
-            result = keep.tile([P, TOKENS], F32, name="result%d" % b)
-            nc.vector.tensor_tensor(
-                out=by_tile(result[:]),
-                in0=by_tile(scaled[:]),
-                in1=u_whole[:].unsqueeze(2).to_broadcast([P, TILES_PER_BATCH, P]),
-                op=ALU.mult,
-            )
+        def sinkhorn_steps(b, pool, bank_name):
+            state = {}
+
+            def nothing():
+                return
+
+            def first_token_step():
+                column_sum = vectors.tile([P, 1], F32, name="column_sum%d" % b)
+                nc.vector.reduce_sum(out=column_sum[:], in_=group_sums[b][:], axis=mybir.AxisListType.X)
+                state["v"] = pair_of_reciprocal(column_sum[:], 1, "v%d" % b)
+
+            def multiply_by_v():
+                v_whole, v_hi, v_lo = state["v"]
+                bank = pool.tile([P, BANK_WORDS], F32, name=bank_name)
+                for c in range(TILES_PER_BATCH):
+                    cols = slice(c * P, (c + 1) * P)
+                    terms = [(hi_by_expert, v_hi), (lo_by_expert, v_hi), (hi_by_expert, v_lo)]
+                    for t in range(len(terms)):
+                        matrix, vector = terms[t]
+                        nc.tensor.matmul(
+                            out=bank[:, c * REPEAT : (c + 1) * REPEAT],
+                            lhsT=matrix[b][:, cols],
+                            rhs=vector[:, 0:1].to_broadcast([P, REPEAT]),
+                            start=(t == 0),
+                            stop=(t == len(terms) - 1),
+                        )
+                state["bank"] = bank
+
+            def take_u():
+                sums = state["bank"][:, 0 : TILES_PER_BATCH * REPEAT : REPEAT]
+                state["u"] = pair_of_reciprocal(sums, TILES_PER_BATCH, "u%d" % b)
+
+            def multiply_by_u():
+                u_whole, u_hi, u_lo = state["u"]
+                bank = pool.tile([P, BANK_WORDS], F32, name=bank_name)
+                terms = []
+                for matrix, vector in ((hi_by_token, u_hi), (lo_by_token, u_hi), (hi_by_token, u_lo)):
+                    for c in range(TILES_PER_BATCH):
+                        terms.append((matrix, vector, c))
+                for t in range(len(terms)):
+                    matrix, vector, c = terms[t]
+                    nc.tensor.matmul(
+                        out=bank[:, 0:REPEAT],
+                        lhsT=matrix[b][:, c * P : (c + 1) * P],
+                        rhs=vector[:, c : c + 1].to_broadcast([P, REPEAT]),
+                        start=(t == 0),
+                        stop=(t == len(terms) - 1),
+                    )
+                state["bank"] = bank
+
+            def take_v():
+                state["v"] = pair_of_reciprocal(state["bank"][:, 0:1], 1, "v%d" % b)
+
+            def last_product():
+                v_whole, v_hi, v_lo = state["v"]
+                spread = banks.tile([P, BANK_WORDS], F32, name="bank")
+                nc.tensor.transpose(spread[:, 0:P], v_whole[:, 0:1].to_broadcast([P, P]), identity[:])
+                state["spread"] = spread
+                multiply_by_v()
+
+            def result():
+                scaled = keep.tile([P, TOKENS], F32, name="scaled%d" % b)
+                nc.vector.tensor_tensor(
+                    out=by_tile(scaled[:]),
+                    in0=by_tile(k_by_token[b][:]),
+                    in1=state["spread"][:, 0:P].unsqueeze(1).to_broadcast([P, TILES_PER_BATCH, P]),
+                    op=ALU.mult,
+                )
+                u_whole = vectors.tile([P, TILES_PER_BATCH], F32, name="last_u%d" % b)
+                nc.vector.reciprocal(
+                    out=u_whole[:], in_=state["bank"][:, 0 : TILES_PER_BATCH * REPEAT : REPEAT]
+                )
+                result_tile = keep.tile([P, TOKENS], F32, name="result%d" % b)
+                nc.vector.tensor_tensor(
+                    out=by_tile(result_tile[:]),
+                    in0=by_tile(scaled[:]),
+                    in1=u_whole[:].unsqueeze(2).to_broadcast([P, TILES_PER_BATCH, P]),
+                    op=ALU.mult,
+                )
+                result_of[b] = result_tile
+
+            steps = [(nothing, first_token_step)]
+            for r in range(ROUNDS - 1):
+                steps.append((multiply_by_v, take_u))
+                steps.append((multiply_by_u, take_v))
+            steps.append((last_product, result))
+            return steps
+
+        def store(b):
             nc.sync.dma_start(
-                out=out[b].rearrange("(r c) e -> r (c e)", c=TILES_PER_BATCH), in_=result[:]
+                out=out[b].rearrange("(r c) e -> r (c e)", c=TILES_PER_BATCH), in_=result_of[b][:]
             )
+
+        chores = []
+        chores_done = 0
+        early_steps = sinkhorn_steps(0, early_banks, "early_bank")
+        late_steps = sinkhorn_steps(1, banks, "bank")
+        steps_done = 0
+        stored = False
+        result_of = {}
+        multiplied = 0
+        for i in range(len(units) + 2):
+            ready = chores_done >= 3 * GROUPS_PER_BATCH and steps_done < EARLY_STEPS
+            if ready:
+                early_steps[steps_done][0]()
+            if i < len(units):
+                transpose_unit(i)
+            if ready:
+                early_steps[steps_done][1]()
+                steps_done += 1
+            if chores_done < len(chores):
+                chores[chores_done]()
+                chores_done += 1
+            if 0 <= i - 1 < len(units):
+                quantise_unit(i - 1)
+            if (i % RUN == RUN - 1 and i < len(units) - LAST_UNITS) or i >= len(units):
+                for m in range(multiplied, i - 1):
+                    multiply_unit(m)
+                multiplied = max(multiplied, i - 1)
+
+        clamp, turn, split = chores[chores_done:]
+        clamp()
+        late_steps[0][1]()
+        turn()
+        split()
+        for s in range(1, len(late_steps)):
+            late_steps[s][0]()
+            early = steps_done < len(early_steps)
+            if early:
+                early_steps[steps_done][0]()
+            late_steps[s][1]()
+            if early:
+                early_steps[steps_done][1]()
+                steps_done += 1
+            if steps_done == len(early_steps) and not stored:
+                store(0)
+                stored = True
+        store(1)

@@ -9,6 +9,7 @@ U32 = mybir.dt.uint32
 U8 = mybir.dt.uint8
 FP8X4 = mybir.dt.float8_e4m3fn_x4
 ALU = mybir.AluOpType
+ACT = mybir.ActivationFunctionType
 
 P = 128
 PACK = 4
@@ -24,6 +25,9 @@ GROUP = GROUP_TILES * P
 GROUPS_PER_BATCH = TILES_PER_BATCH // GROUP_TILES
 GROUPS = BATCH * GROUPS_PER_BATCH
 PASSES = D // K_PASS
+OUT_HALVES = 2
+OUT_TILES = TILES_PER_BATCH // OUT_HALVES
+OUT_COLS = OUT_TILES * P
 EPS = 1e-6
 ROUNDS = 8
 
@@ -32,13 +36,14 @@ LOAD_PIECES = 16
 SMALL_LOAD_PIECES = 8
 SMALL_LOAD_GROUPS = 3
 SMALLEST_FIRST_LOAD = 4
-SMALLEST_LAST_LOAD = 2
-VECTOR_BANK, BANKS_IN_TURN = 1, 4
+SMALLEST_LAST_LOAD = 1
+VECTOR_BANK, BANKS_IN_TURN = 2, 4
 RUN = 2
-LAST_UNITS = 4
+LAST_UNITS = 5
 EARLY_STEPS = 4
 
-REPEAT = 32
+EARLY_REPEAT = 16
+LATE_REPEAT = 48
 
 FLOPS = 2 * BATCH * TOKENS * D * EXPERTS
 
@@ -47,7 +52,8 @@ def tile_sinkhornrouter_k_kernel(tc, x, w_gate, out):
     nc = tc.nc
     with ExitStack() as stack:
         keep = stack.enter_context(tc.tile_pool(name="keep", bufs=1))
-        raw_pool = stack.enter_context(tc.tile_pool(name="raw", bufs=6))
+        raw_pool = stack.enter_context(tc.tile_pool(name="raw", bufs=4))
+        small_raw_pool = stack.enter_context(tc.tile_pool(name="small_raw", bufs=7))
         grouped_pool = stack.enter_context(tc.tile_pool(name="grouped", bufs=3))
         x_mx_pool = stack.enter_context(tc.tile_pool(name="x_mx", bufs=8))
         vectors = stack.enter_context(tc.tile_pool(name="vectors", bufs=2))
@@ -63,7 +69,6 @@ def tile_sinkhornrouter_k_kernel(tc, x, w_gate, out):
         w_scales = keep.tile([P, PASSES * EXPERTS], U8, name="w_scales", align_bytes=64)
 
         k_by_expert = [keep.tile([P, TOKENS], F32, name="k_by_expert%d" % b) for b in range(BATCH)]
-        k_by_token = [keep.tile([P, TOKENS], F32, name="k_by_token%d" % b) for b in range(BATCH)]
         group_sums = [keep.tile([P, GROUPS_PER_BATCH], F32, name="group_sums%d" % b) for b in range(BATCH)]
         hi_by_expert = [keep.tile([P, TOKENS], BF16, name="hi_by_expert%d" % b) for b in range(BATCH)]
         lo_by_expert = [keep.tile([P, TOKENS], BF16, name="lo_by_expert%d" % b) for b in range(BATCH)]
@@ -120,7 +125,10 @@ def tile_sinkhornrouter_k_kernel(tc, x, w_gate, out):
             n, tiles, j, first, passes, inside = units[i]
             rows, tiles, j, load_first, load_passes = loads[n]
             if inside == 0:
-                raw = raw_pool.tile([P, LOAD_PIECES * K_PASS], BF16, name="raw")
+                if tiles * load_passes <= SMALL_LOAD_PIECES:
+                    raw = small_raw_pool.tile([P, SMALL_LOAD_PIECES * K_PASS], BF16, name="small_raw")
+                else:
+                    raw = raw_pool.tile([P, LOAD_PIECES * K_PASS], BF16, name="raw")
                 nc.sync.dma_start(
                     out=raw[:, 0 : tiles * load_passes * K_PASS].rearrange("p (c d) -> p c d", c=tiles),
                     in_=rows[:, :, load_first * K_PASS : (load_first + load_passes) * K_PASS],
@@ -129,18 +137,20 @@ def tile_sinkhornrouter_k_kernel(tc, x, w_gate, out):
             raw_words = raw_of[n][:].bitcast(F32)
             grouped = grouped_pool.tile([P, UNIT_PIECES * P * PACK], BF16, name="grouped", align_bytes=64)
             grouped_words = grouped[:].bitcast(F32).rearrange("p (s r u) -> p s r u", s=UNIT_PIECES, u=HALVES)
-            for k in range(passes * tiles // BANK_PIECES):
+            pieces = passes * tiles
+            in_bank = BANK_PIECES if pieces > BANK_PIECES else 1
+            for k in range(pieces // in_bank):
                 bank = banks.tile([P, BANK_WORDS], F32, name="bank")
-                for t in range(BANK_PIECES):
-                    g, c = divmod(k * BANK_PIECES + t, tiles)
+                for t in range(in_bank):
+                    g, c = divmod(k * in_bank + t, tiles)
                     for u in range(HALVES):
                         word = ((c * load_passes + inside + g) * HALVES + u) * P
                         at = (t * HALVES + u) * P
                         nc.tensor.transpose(bank[:, at : at + P], raw_words[:, word : word + P], identity[:])
                 copy = nc.vector.tensor_copy if k % BANKS_IN_TURN == VECTOR_BANK else nc.scalar.copy
                 copy(
-                    out=grouped_words[:, k * BANK_PIECES : (k + 1) * BANK_PIECES, :, :],
-                    in_=bank[:].rearrange("p (s u r) -> p s r u", s=BANK_PIECES, u=HALVES),
+                    out=grouped_words[:, k * in_bank : (k + 1) * in_bank, :, :],
+                    in_=bank[:, 0 : in_bank * HALVES * P].rearrange("p (s u r) -> p s r u", s=in_bank, u=HALVES),
                 )
             grouped_of[i] = grouped
 
@@ -184,6 +194,7 @@ def tile_sinkhornrouter_k_kernel(tc, x, w_gate, out):
         def group_chores(j):
             b, q = divmod(j, GROUPS_PER_BATCH)
             cols = slice(q * GROUP, (q + 1) * GROUP)
+            turned = {}
 
             def clamp():
                 nc.vector.tensor_scalar(
@@ -205,15 +216,15 @@ def tile_sinkhornrouter_k_kernel(tc, x, w_gate, out):
                         bank[:, c * P : (c + 1) * P], k_by_expert[b][:, at : at + P], identity[:]
                     )
                 nc.scalar.copy(out=hi_by_token[b][:, cols], in_=bank[:, 0:GROUP])
-                nc.scalar.copy(out=k_by_token[b][:, cols], in_=bank[:, 0:GROUP])
+                turned["bank"] = bank
 
             def split():
                 for lo, whole, hi in (
-                    (lo_by_expert, k_by_expert, hi_by_expert),
-                    (lo_by_token, k_by_token, hi_by_token),
+                    (lo_by_expert, k_by_expert[b][:, cols], hi_by_expert),
+                    (lo_by_token, turned["bank"][:, 0:GROUP], hi_by_token),
                 ):
                     nc.vector.tensor_tensor(
-                        out=lo[b][:, cols], in0=whole[b][:, cols], in1=hi[b][:, cols], op=ALU.subtract
+                        out=lo[b][:, cols], in0=whole, in1=hi[b][:, cols], op=ALU.subtract
                     )
 
             return [clamp, turn, split]
@@ -226,10 +237,7 @@ def tile_sinkhornrouter_k_kernel(tc, x, w_gate, out):
             nc.vector.tensor_tensor(out=lo[:], in0=whole[:], in1=hi, op=ALU.subtract)
             return whole, hi, lo[:]
 
-        def by_tile(ap):
-            return ap.rearrange("p (c e) -> p c e", c=TILES_PER_BATCH)
-
-        def sinkhorn_steps(b, pool, bank_name):
+        def sinkhorn_steps(b, pool, bank_name, repeat):
             state = {}
 
             def nothing():
@@ -249,16 +257,16 @@ def tile_sinkhornrouter_k_kernel(tc, x, w_gate, out):
                     for t in range(len(terms)):
                         matrix, vector = terms[t]
                         nc.tensor.matmul(
-                            out=bank[:, c * REPEAT : (c + 1) * REPEAT],
+                            out=bank[:, c * repeat : (c + 1) * repeat],
                             lhsT=matrix[b][:, cols],
-                            rhs=vector[:, 0:1].to_broadcast([P, REPEAT]),
+                            rhs=vector[:, 0:1].to_broadcast([P, repeat]),
                             start=(t == 0),
                             stop=(t == len(terms) - 1),
                         )
                 state["bank"] = bank
 
             def take_u():
-                sums = state["bank"][:, 0 : TILES_PER_BATCH * REPEAT : REPEAT]
+                sums = state["bank"][:, 0 : TILES_PER_BATCH * repeat : repeat]
                 state["u"] = pair_of_reciprocal(sums, TILES_PER_BATCH, "u%d" % b)
 
             def multiply_by_u():
@@ -271,9 +279,9 @@ def tile_sinkhornrouter_k_kernel(tc, x, w_gate, out):
                 for t in range(len(terms)):
                     matrix, vector, c = terms[t]
                     nc.tensor.matmul(
-                        out=bank[:, 0:REPEAT],
+                        out=bank[:, 0:repeat],
                         lhsT=matrix[b][:, c * P : (c + 1) * P],
-                        rhs=vector[:, c : c + 1].to_broadcast([P, REPEAT]),
+                        rhs=vector[:, c : c + 1].to_broadcast([P, repeat]),
                         start=(t == 0),
                         stop=(t == len(terms) - 1),
                     )
@@ -282,56 +290,66 @@ def tile_sinkhornrouter_k_kernel(tc, x, w_gate, out):
             def take_v():
                 state["v"] = pair_of_reciprocal(state["bank"][:, 0:1], 1, "v%d" % b)
 
-            def last_product():
+            def scale_by_v():
                 v_whole, v_hi, v_lo = state["v"]
-                spread = banks.tile([P, BANK_WORDS], F32, name="bank")
-                nc.tensor.transpose(spread[:, 0:P], v_whole[:, 0:1].to_broadcast([P, P]), identity[:])
-                state["spread"] = spread
-                multiply_by_v()
-
-            def result():
-                scaled = keep.tile([P, TOKENS], F32, name="scaled%d" % b)
-                nc.vector.tensor_tensor(
-                    out=by_tile(scaled[:]),
-                    in0=by_tile(k_by_token[b][:]),
-                    in1=state["spread"][:, 0:P].unsqueeze(1).to_broadcast([P, TILES_PER_BATCH, P]),
-                    op=ALU.mult,
-                )
+                for h in range(OUT_HALVES):
+                    cols = slice(h * OUT_COLS, (h + 1) * OUT_COLS)
+                    scaled = keep.tile([P, OUT_COLS], F32, name="scaled%d%d" % (b, h))
+                    nc.vector.tensor_scalar(
+                        out=scaled[:], in0=k_by_expert[b][:, cols], scalar1=v_whole[:, 0:1], scalar2=None, op0=ALU.mult
+                    )
+                    state["scaled", h] = scaled
                 u_whole = vectors.tile([P, TILES_PER_BATCH], F32, name="last_u%d" % b)
                 nc.vector.reciprocal(
-                    out=u_whole[:], in_=state["bank"][:, 0 : TILES_PER_BATCH * REPEAT : REPEAT]
+                    out=u_whole[:], in_=state["bank"][:, 0 : TILES_PER_BATCH * repeat : repeat]
                 )
-                result_tile = keep.tile([P, TOKENS], F32, name="result%d" % b)
-                nc.vector.tensor_tensor(
-                    out=by_tile(result_tile[:]),
-                    in0=by_tile(scaled[:]),
-                    in1=u_whole[:].unsqueeze(2).to_broadcast([P, TILES_PER_BATCH, P]),
-                    op=ALU.mult,
-                )
-                result_of[b] = result_tile
+                state["u"] = u_whole
+
+            def turn_scaled():
+                for h in range(OUT_HALVES):
+                    bank = banks.tile([P, BANK_WORDS], F32, name="bank")
+                    for c in range(OUT_TILES):
+                        at = slice(c * P, (c + 1) * P)
+                        nc.tensor.transpose(bank[:, at], state["scaled", h][:, at], identity[:])
+                    state["turned", h] = bank
+
+            def result():
+                for h in range(OUT_HALVES):
+                    done = keep.tile([P, OUT_COLS], F32, name="result%d%d" % (b, h))
+                    for c in range(OUT_TILES):
+                        at = slice(c * P, (c + 1) * P)
+                        u = state["u"][:, h * OUT_TILES + c : h * OUT_TILES + c + 1]
+                        if h == 0:
+                            nc.vector.tensor_scalar(
+                                out=done[:, at], in0=state["turned", h][:, at], scalar1=u, scalar2=None, op0=ALU.mult
+                            )
+                        else:
+                            nc.scalar.activation(
+                                out=done[:, at], in_=state["turned", h][:, at], func=ACT.Copy, scale=u
+                            )
+                    rows = out[b].rearrange("(r h c) e -> h r (c e)", h=OUT_HALVES, c=OUT_TILES)
+                    queue = nc.sync if h == 0 else nc.scalar
+                    queue.dma_start(out=rows[h], in_=done[:])
 
             steps = [(nothing, first_token_step)]
             for r in range(ROUNDS - 1):
                 steps.append((multiply_by_v, take_u))
                 steps.append((multiply_by_u, take_v))
-            steps.append((last_product, result))
+            steps.append((multiply_by_v, scale_by_v))
+            steps.append((turn_scaled, result))
             return steps
-
-        def store(b):
-            nc.sync.dma_start(
-                out=out[b].rearrange("(r c) e -> r (c e)", c=TILES_PER_BATCH), in_=result_of[b][:]
-            )
 
         chores = []
         chores_done = 0
-        early_steps = sinkhorn_steps(0, early_banks, "early_bank")
-        late_steps = sinkhorn_steps(1, banks, "bank")
+        early_steps = sinkhorn_steps(0, early_banks, "early_bank", EARLY_REPEAT)
+        late_steps = sinkhorn_steps(1, banks, "bank", LATE_REPEAT)
         steps_done = 0
-        stored = False
-        result_of = {}
         multiplied = 0
         for i in range(len(units) + 2):
             ready = chores_done >= 3 * GROUPS_PER_BATCH and steps_done < EARLY_STEPS
+            if chores_done < len(chores):
+                chores[chores_done]()
+                chores_done += 1
             if ready:
                 early_steps[steps_done][0]()
             if i < len(units):
@@ -339,9 +357,6 @@ def tile_sinkhornrouter_k_kernel(tc, x, w_gate, out):
             if ready:
                 early_steps[steps_done][1]()
                 steps_done += 1
-            if chores_done < len(chores):
-                chores[chores_done]()
-                chores_done += 1
             if 0 <= i - 1 < len(units):
                 quantise_unit(i - 1)
             if (i % RUN == RUN - 1 and i < len(units) - LAST_UNITS) or i >= len(units):
@@ -363,7 +378,3 @@ def tile_sinkhornrouter_k_kernel(tc, x, w_gate, out):
             if early:
                 early_steps[steps_done][1]()
                 steps_done += 1
-            if steps_done == len(early_steps) and not stored:
-                store(0)
-                stored = True
-        store(1)

@@ -36,14 +36,14 @@ LOAD_PIECES = 16
 SMALL_LOAD_PIECES = 8
 SMALL_LOAD_GROUPS = 3
 SMALLEST_FIRST_LOAD = 4
-SMALLEST_LAST_LOAD = 1
-VECTOR_BANK, BANKS_IN_TURN = 2, 4
+SMALLEST_LAST_LOAD = 2
+VECTOR_BANK, BANKS_IN_TURN = 1, 4
 RUN = 2
-LAST_UNITS = 5
+LAST_UNITS = 4
 EARLY_STEPS = 4
 
-EARLY_REPEAT = 16
-LATE_REPEAT = 48
+EARLY_REPEAT = 32
+LATE_REPEAT = 32
 
 FLOPS = 2 * BATCH * TOKENS * D * EXPERTS
 
@@ -52,8 +52,7 @@ def tile_sinkhornrouter_k_kernel(tc, x, w_gate, out):
     nc = tc.nc
     with ExitStack() as stack:
         keep = stack.enter_context(tc.tile_pool(name="keep", bufs=1))
-        raw_pool = stack.enter_context(tc.tile_pool(name="raw", bufs=4))
-        small_raw_pool = stack.enter_context(tc.tile_pool(name="small_raw", bufs=7))
+        raw_pool = stack.enter_context(tc.tile_pool(name="raw", bufs=6))
         grouped_pool = stack.enter_context(tc.tile_pool(name="grouped", bufs=3))
         x_mx_pool = stack.enter_context(tc.tile_pool(name="x_mx", bufs=8))
         vectors = stack.enter_context(tc.tile_pool(name="vectors", bufs=2))
@@ -125,10 +124,7 @@ def tile_sinkhornrouter_k_kernel(tc, x, w_gate, out):
             n, tiles, j, first, passes, inside = units[i]
             rows, tiles, j, load_first, load_passes = loads[n]
             if inside == 0:
-                if tiles * load_passes <= SMALL_LOAD_PIECES:
-                    raw = small_raw_pool.tile([P, SMALL_LOAD_PIECES * K_PASS], BF16, name="small_raw")
-                else:
-                    raw = raw_pool.tile([P, LOAD_PIECES * K_PASS], BF16, name="raw")
+                raw = raw_pool.tile([P, LOAD_PIECES * K_PASS], BF16, name="raw")
                 nc.sync.dma_start(
                     out=raw[:, 0 : tiles * load_passes * K_PASS].rearrange("p (c d) -> p c d", c=tiles),
                     in_=rows[:, :, load_first * K_PASS : (load_first + load_passes) * K_PASS],
@@ -138,7 +134,7 @@ def tile_sinkhornrouter_k_kernel(tc, x, w_gate, out):
             grouped = grouped_pool.tile([P, UNIT_PIECES * P * PACK], BF16, name="grouped", align_bytes=64)
             grouped_words = grouped[:].bitcast(F32).rearrange("p (s r u) -> p s r u", s=UNIT_PIECES, u=HALVES)
             pieces = passes * tiles
-            in_bank = BANK_PIECES if pieces > BANK_PIECES else 1
+            in_bank = min(BANK_PIECES, pieces)
             for k in range(pieces // in_bank):
                 bank = banks.tile([P, BANK_WORDS], F32, name="bank")
                 for t in range(in_bank):
@@ -328,8 +324,7 @@ def tile_sinkhornrouter_k_kernel(tc, x, w_gate, out):
                                 out=done[:, at], in_=state["turned", h][:, at], func=ACT.Copy, scale=u
                             )
                     rows = out[b].rearrange("(r h c) e -> h r (c e)", h=OUT_HALVES, c=OUT_TILES)
-                    queue = nc.sync if h == 0 else nc.scalar
-                    queue.dma_start(out=rows[h], in_=done[:])
+                    nc.sync.dma_start(out=rows[h], in_=done[:])
 
             steps = [(nothing, first_token_step)]
             for r in range(ROUNDS - 1):

@@ -247,18 +247,19 @@ def tile_sinkhornrouter_k_kernel(tc, x, w_gate, out):
             def multiply_by_v():
                 v_whole, v_hi, v_lo = state["v"]
                 bank = pool.tile([P, BANK_WORDS], F32, name=bank_name)
-                for c in range(TILES_PER_BATCH):
-                    cols = slice(c * P, (c + 1) * P)
-                    terms = [(hi_by_expert, v_hi), (lo_by_expert, v_hi), (hi_by_expert, v_lo)]
-                    for t in range(len(terms)):
-                        matrix, vector = terms[t]
-                        nc.tensor.matmul(
-                            out=bank[:, c * repeat : (c + 1) * repeat],
-                            lhsT=matrix[b][:, cols],
-                            rhs=vector[:, 0:1].to_broadcast([P, repeat]),
-                            start=(t == 0),
-                            stop=(t == len(terms) - 1),
-                        )
+                terms = []
+                for matrix, vector in ((hi_by_expert, v_hi), (lo_by_expert, v_hi), (hi_by_expert, v_lo)):
+                    for c in range(TILES_PER_BATCH):
+                        terms.append((matrix, vector, c))
+                for t in range(len(terms)):
+                    matrix, vector, c = terms[t]
+                    nc.tensor.matmul(
+                        out=bank[:, c * repeat : (c + 1) * repeat],
+                        lhsT=matrix[b][:, c * P : (c + 1) * P],
+                        rhs=vector[:, 0:1].to_broadcast([P, repeat]),
+                        start=(t == 0),
+                        stop=(t == len(terms) - 1),
+                    )
                 state["bank"] = bank
 
             def take_u():

@@ -34,16 +34,17 @@ ROUNDS = 8
 UNIT_PIECES = 8
 LOAD_PIECES = 16
 SMALL_LOAD_PIECES = 8
-SMALL_LOAD_GROUPS = 3
+SMALL_LOAD_GROUPS = 5
 SMALLEST_FIRST_LOAD = 4
 SMALLEST_LAST_LOAD = 2
-VECTOR_BANK, BANKS_IN_TURN = 1, 4
+VECTOR_BANK, BANKS_IN_TURN = 2, 4
 RUN = 2
+SINGLE_RUNS = 12
 LAST_UNITS = 4
-EARLY_STEPS = 4
+EARLY_STEPS = 2
 
-EARLY_REPEAT = 32
-LATE_REPEAT = 32
+REPEAT = 32
+LONE_REPEAT = 48
 
 FLOPS = 2 * BATCH * TOKENS * D * EXPERTS
 
@@ -233,8 +234,13 @@ def tile_sinkhornrouter_k_kernel(tc, x, w_gate, out):
             nc.vector.tensor_tensor(out=lo[:], in0=whole[:], in1=hi, op=ALU.subtract)
             return whole, hi, lo[:]
 
-        def sinkhorn_steps(b, pool, bank_name, repeat):
-            state = {}
+        def sinkhorn_steps(b, pool, bank_name, lone):
+            state = {"products": 0}
+
+            def next_repeat():
+                state["products"] += 1
+                state["repeat"] = LONE_REPEAT if state["products"] > 2 * ROUNDS - 1 - lone else REPEAT
+                return state["repeat"]
 
             def nothing():
                 return
@@ -246,6 +252,7 @@ def tile_sinkhornrouter_k_kernel(tc, x, w_gate, out):
 
             def multiply_by_v():
                 v_whole, v_hi, v_lo = state["v"]
+                repeat = next_repeat()
                 bank = pool.tile([P, BANK_WORDS], F32, name=bank_name)
                 terms = []
                 for matrix, vector in ((hi_by_expert, v_hi), (lo_by_expert, v_hi), (hi_by_expert, v_lo)):
@@ -263,11 +270,13 @@ def tile_sinkhornrouter_k_kernel(tc, x, w_gate, out):
                 state["bank"] = bank
 
             def take_u():
+                repeat = state["repeat"]
                 sums = state["bank"][:, 0 : TILES_PER_BATCH * repeat : repeat]
                 state["u"] = pair_of_reciprocal(sums, TILES_PER_BATCH, "u%d" % b)
 
             def multiply_by_u():
                 u_whole, u_hi, u_lo = state["u"]
+                repeat = next_repeat()
                 bank = pool.tile([P, BANK_WORDS], F32, name=bank_name)
                 terms = []
                 for matrix, vector in ((hi_by_token, u_hi), (lo_by_token, u_hi), (hi_by_token, u_lo)):
@@ -289,6 +298,7 @@ def tile_sinkhornrouter_k_kernel(tc, x, w_gate, out):
 
             def scale_by_v():
                 v_whole, v_hi, v_lo = state["v"]
+                repeat = state["repeat"]
                 for h in range(OUT_HALVES):
                     cols = slice(h * OUT_COLS, (h + 1) * OUT_COLS)
                     scaled = keep.tile([P, OUT_COLS], F32, name="scaled%d%d" % (b, h))
@@ -337,8 +347,8 @@ def tile_sinkhornrouter_k_kernel(tc, x, w_gate, out):
 
         chores = []
         chores_done = 0
-        early_steps = sinkhorn_steps(0, early_banks, "early_bank", EARLY_REPEAT)
-        late_steps = sinkhorn_steps(1, banks, "bank", LATE_REPEAT)
+        early_steps = sinkhorn_steps(0, early_banks, "early_bank", 0)
+        late_steps = sinkhorn_steps(1, banks, "bank", EARLY_STEPS - 1)
         steps_done = 0
         multiplied = 0
         for i in range(len(units) + 2):
@@ -355,7 +365,8 @@ def tile_sinkhornrouter_k_kernel(tc, x, w_gate, out):
                 steps_done += 1
             if 0 <= i - 1 < len(units):
                 quantise_unit(i - 1)
-            if (i % RUN == RUN - 1 and i < len(units) - LAST_UNITS) or i >= len(units):
+            left = len(units) - i
+            if (i % RUN == RUN - 1 or left <= SINGLE_RUNS) and left > LAST_UNITS or left <= 0:
                 for m in range(multiplied, i - 1):
                     multiply_unit(m)
                 multiplied = max(multiplied, i - 1)

@@ -37,7 +37,7 @@ SMALL_LOAD_PIECES = 8
 SMALL_LOAD_GROUPS = 5
 SMALLEST_FIRST_LOAD = 4
 SMALLEST_LAST_LOAD = 2
-VECTOR_BANK, BANKS_IN_TURN = 2, 4
+VECTOR_BANK, BANKS_IN_TURN = 1, 4
 RUN = 2
 SINGLE_RUNS = 12
 LAST_UNITS = 4
@@ -54,12 +54,11 @@ def tile_sinkhornrouter_k_kernel(tc, x, w_gate, out):
     with ExitStack() as stack:
         keep = stack.enter_context(tc.tile_pool(name="keep", bufs=1))
         raw_pool = stack.enter_context(tc.tile_pool(name="raw", bufs=6))
-        grouped_pool = stack.enter_context(tc.tile_pool(name="grouped", bufs=3))
+        grouped_pool = stack.enter_context(tc.tile_pool(name="grouped", bufs=4))
         x_mx_pool = stack.enter_context(tc.tile_pool(name="x_mx", bufs=8))
         vectors = stack.enter_context(tc.tile_pool(name="vectors", bufs=2))
-        banks = stack.enter_context(tc.psum_pool(name="banks", bufs=5))
+        banks = stack.enter_context(tc.psum_pool(name="banks", bufs=6))
         gate_banks = stack.enter_context(tc.psum_pool(name="gate_banks", bufs=2))
-        early_banks = stack.enter_context(tc.psum_pool(name="early_banks", bufs=1))
         stack.enter_context(tc.manual_schedule())
 
         identity = keep.tile([P, P], F32, name="identity")
@@ -144,7 +143,8 @@ def tile_sinkhornrouter_k_kernel(tc, x, w_gate, out):
                         word = ((c * load_passes + inside + g) * HALVES + u) * P
                         at = (t * HALVES + u) * P
                         nc.tensor.transpose(bank[:, at : at + P], raw_words[:, word : word + P], identity[:])
-                copy = nc.vector.tensor_copy if k % BANKS_IN_TURN == VECTOR_BANK else nc.scalar.copy
+                by_vector = k % BANKS_IN_TURN == VECTOR_BANK and i < len(units) - LAST_UNITS
+                copy = nc.vector.tensor_copy if by_vector else nc.scalar.copy
                 copy(
                     out=grouped_words[:, k * in_bank : (k + 1) * in_bank, :, :],
                     in_=bank[:, 0 : in_bank * HALVES * P].rearrange("p (s u r) -> p s r u", s=in_bank, u=HALVES),
@@ -234,7 +234,7 @@ def tile_sinkhornrouter_k_kernel(tc, x, w_gate, out):
             nc.vector.tensor_tensor(out=lo[:], in0=whole[:], in1=hi, op=ALU.subtract)
             return whole, hi, lo[:]
 
-        def sinkhorn_steps(b, pool, bank_name, lone):
+        def sinkhorn_steps(b, lone):
             state = {"products": 0}
 
             def next_repeat():
@@ -253,7 +253,7 @@ def tile_sinkhornrouter_k_kernel(tc, x, w_gate, out):
             def multiply_by_v():
                 v_whole, v_hi, v_lo = state["v"]
                 repeat = next_repeat()
-                bank = pool.tile([P, BANK_WORDS], F32, name=bank_name)
+                bank = banks.tile([P, BANK_WORDS], F32, name="bank")
                 terms = []
                 for matrix, vector in ((hi_by_expert, v_hi), (lo_by_expert, v_hi), (hi_by_expert, v_lo)):
                     for c in range(TILES_PER_BATCH):
@@ -277,7 +277,7 @@ def tile_sinkhornrouter_k_kernel(tc, x, w_gate, out):
             def multiply_by_u():
                 u_whole, u_hi, u_lo = state["u"]
                 repeat = next_repeat()
-                bank = pool.tile([P, BANK_WORDS], F32, name=bank_name)
+                bank = banks.tile([P, BANK_WORDS], F32, name="bank")
                 terms = []
                 for matrix, vector in ((hi_by_token, u_hi), (lo_by_token, u_hi), (hi_by_token, u_lo)):
                     for c in range(TILES_PER_BATCH):
@@ -347,8 +347,8 @@ def tile_sinkhornrouter_k_kernel(tc, x, w_gate, out):
 
         chores = []
         chores_done = 0
-        early_steps = sinkhorn_steps(0, early_banks, "early_bank", 0)
-        late_steps = sinkhorn_steps(1, banks, "bank", EARLY_STEPS - 1)
+        early_steps = sinkhorn_steps(0, 0)
+        late_steps = sinkhorn_steps(1, EARLY_STEPS - 1)
         steps_done = 0
         multiplied = 0
         for i in range(len(units) + 2):

from contextlib import ExitStack

import concourse.mybir as mybir
from concourse.masks import make_identity

F32 = mybir.dt.float32
BF16 = mybir.dt.bfloat16
U32 = mybir.dt.uint32
U8 = mybir.dt.uint8
FP8X4 = mybir.dt.float8_e4m3fn_x4
ALU = mybir.AluOpType
ACT = mybir.ActivationFunctionType

P = 128
PACK = 4
K_PASS = P * PACK
HALVES = 2
BANK_WORDS = 512
BANK_PIECES = BANK_WORDS // (HALVES * P)

BATCH, TOKENS, D, EXPERTS = 2, 512, 16384, 128
TILES_PER_BATCH = TOKENS // P
GROUP_TILES = 1
GROUP = GROUP_TILES * P
GROUPS_PER_BATCH = TILES_PER_BATCH // GROUP_TILES
GROUPS = BATCH * GROUPS_PER_BATCH
PASSES = D // K_PASS
OUT_HALVES = 2
OUT_TILES = TILES_PER_BATCH // OUT_HALVES
OUT_COLS = OUT_TILES * P
EPS = 1e-6
ROUNDS = 8

UNIT_PIECES = 8
LOAD_PIECES = 16
SMALL_LOAD_PIECES = 8
SMALL_LOAD_GROUPS = 5
SMALLEST_FIRST_LOAD = 4
SMALLEST_LAST_LOAD = 2
VECTOR_BANK, BANKS_IN_TURN = 1, 4
RUN = 2
SINGLE_RUNS = 12
LAST_UNITS = 4
EARLY_STEPS = 2

REPEAT = 32
LONE_REPEAT = 48

FLOPS = 2 * BATCH * TOKENS * D * EXPERTS


def tile_sinkhornrouter_k_kernel(tc, x, w_gate, out):
    nc = tc.nc
    with ExitStack() as stack:
        keep = stack.enter_context(tc.tile_pool(name="keep", bufs=1))
        raw_pool = stack.enter_context(tc.tile_pool(name="raw", bufs=6))
        grouped_pool = stack.enter_context(tc.tile_pool(name="grouped", bufs=4))
        x_mx_pool = stack.enter_context(tc.tile_pool(name="x_mx", bufs=8))
        vectors = stack.enter_context(tc.tile_pool(name="vectors", bufs=2))
        banks = stack.enter_context(tc.psum_pool(name="banks", bufs=6))
        gate_banks = stack.enter_context(tc.psum_pool(name="gate_banks", bufs=2))
        stack.enter_context(tc.manual_schedule())

        identity = keep.tile([P, P], F32, name="identity")
        make_identity(nc, identity[:])

        w_codes = keep.tile([P, PASSES * EXPERTS], U32, name="w_codes", align_bytes=64)
        w_scales = keep.tile([P, PASSES * EXPERTS], U8, name="w_scales", align_bytes=64)

        k_by_expert = [keep.tile([P, TOKENS], F32, name="k_by_expert%d" % b) for b in range(BATCH)]
        group_sums = [keep.tile([P, GROUPS_PER_BATCH], F32, name="group_sums%d" % b) for b in range(BATCH)]
        hi_by_expert = [keep.tile([P, TOKENS], BF16, name="hi_by_expert%d" % b) for b in range(BATCH)]
        lo_by_expert = [keep.tile([P, TOKENS], BF16, name="lo_by_expert%d" % b) for b in range(BATCH)]
        hi_by_token = [keep.tile([P, TOKENS], BF16, name="hi_by_token%d" % b) for b in range(BATCH)]
        lo_by_token = [keep.tile([P, TOKENS], BF16, name="lo_by_token%d" % b) for b in range(BATCH)]

        w_rows = w_gate.rearrange("(r c) d -> r c d", c=1)
        group_rows = []
        for b in range(BATCH):
            by_row = x[b].rearrange("(r c) d -> r c d", c=TILES_PER_BATCH)
            for c in range(0, TILES_PER_BATCH, GROUP_TILES):
                group_rows.append(by_row[:, c : c + GROUP_TILES, :])

        def cuts(total, most, smallest):
            sizes = []
            left = total
            while left > most:
                sizes.append(most)
                left -= most
            while left > smallest:
                sizes.append(left // 2)
                left -= left // 2
            sizes.append(left)
            return sizes

        loads = []
        for j in range(GROUPS):
            most = LOAD_PIECES if j < GROUPS - SMALL_LOAD_GROUPS else SMALL_LOAD_PIECES
            sizes = cuts(PASSES, most // GROUP_TILES, PASSES)
            if j == 0:
                sizes = list(reversed(cuts(PASSES, most // GROUP_TILES, SMALLEST_FIRST_LOAD)))
            if j == GROUPS - 1:
                sizes = cuts(PASSES, most // GROUP_TILES, SMALLEST_LAST_LOAD // GROUP_TILES)
            first = 0
            for passes in sizes:
                if j == 0:
                    loads.append((w_rows, 1, None, first, passes))
                loads.append((group_rows[j], GROUP_TILES, j, first, passes))
                first += passes

        units = []
        for n in range(len(loads)):
            rows, tiles, j, first, passes = loads[n]
            step = UNIT_PIECES // tiles
            for inside in range(0, passes, step):
                units.append((n, tiles, j, first + inside, min(step, passes - inside), inside))

        raw_of = {}
        grouped_of = {}
        mx_of = {}
        gates_of = {}

        def transpose_unit(i):
            n, tiles, j, first, passes, inside = units[i]
            rows, tiles, j, load_first, load_passes = loads[n]
            if inside == 0:
                raw = raw_pool.tile([P, LOAD_PIECES * K_PASS], BF16, name="raw")
                nc.sync.dma_start(
                    out=raw[:, 0 : tiles * load_passes * K_PASS].rearrange("p (c d) -> p c d", c=tiles),
                    in_=rows[:, :, load_first * K_PASS : (load_first + load_passes) * K_PASS],
                )
                raw_of[n] = raw
            raw_words = raw_of[n][:].bitcast(F32)
            grouped = grouped_pool.tile([P, UNIT_PIECES * P * PACK], BF16, name="grouped", align_bytes=64)
            grouped_words = grouped[:].bitcast(F32).rearrange("p (s r u) -> p s r u", s=UNIT_PIECES, u=HALVES)
            pieces = passes * tiles
            in_bank = min(BANK_PIECES, pieces)
            for k in range(pieces // in_bank):
                bank = banks.tile([P, BANK_WORDS], F32, name="bank")
                for t in range(in_bank):
                    g, c = divmod(k * in_bank + t, tiles)
                    for u in range(HALVES):
                        word = ((c * load_passes + inside + g) * HALVES + u) * P
                        at = (t * HALVES + u) * P
                        nc.tensor.transpose(bank[:, at : at + P], raw_words[:, word : word + P], identity[:])
                by_vector = k % BANKS_IN_TURN == VECTOR_BANK and i < len(units) - LAST_UNITS
                copy = nc.vector.tensor_copy if by_vector else nc.scalar.copy
                copy(
                    out=grouped_words[:, k * in_bank : (k + 1) * in_bank, :, :],
                    in_=bank[:, 0 : in_bank * HALVES * P].rearrange("p (s u r) -> p s r u", s=in_bank, u=HALVES),
                )
            grouped_of[i] = grouped

        def quantise_unit(i):
            n, tiles, j, first, passes, inside = units[i]
            columns = passes * tiles * P
            if j is None:
                cols = slice(first * P, (first + passes) * P)
                codes, scales = w_codes[:, cols], w_scales[:, cols]
            else:
                x_codes = x_mx_pool.tile([P, UNIT_PIECES * P], U32, name="x_codes", align_bytes=64)
                x_scales = x_mx_pool.tile([P, UNIT_PIECES * P], U8, name="x_scales", align_bytes=64)
                codes, scales = x_codes[:, 0:columns], x_scales[:, 0:columns]
                mx_of[i] = (codes, scales)
            nc.vector.quantize_mx(
                out=codes.bitcast(FP8X4), scales=scales, in_=grouped_of[i][:, 0 : columns * PACK]
            )

        def multiply_unit(i):
            n, tiles, j, first, passes, inside = units[i]
            if j is None:
                return
            if first == 0:
                gates_of[j] = gate_banks.tile([P, BANK_WORDS], F32, name="gates")
            codes, scales = mx_of[i]
            for g in range(passes):
                w_cols = slice((first + g) * P, (first + g + 1) * P)
                x_cols = slice(g * GROUP, (g + 1) * GROUP)
                nc.tensor.matmul_mx(
                    out=gates_of[j][:, 0:GROUP],
                    lhsT=w_codes[:, w_cols].bitcast(FP8X4),
                    lhsT_scale=w_scales[:, w_cols],
                    rhs=codes[:, x_cols].bitcast(FP8X4),
                    rhs_scale=scales[:, x_cols],
                    start=(first + g == 0),
                    stop=(first + g == PASSES - 1),
                )
            if first + passes == PASSES:
                chores.extend(group_chores(j))

        def group_chores(j):
            b, q = divmod(j, GROUPS_PER_BATCH)
            cols = slice(q * GROUP, (q + 1) * GROUP)
            turned = {}

            def clamp():
                nc.vector.tensor_scalar(
                    out=k_by_expert[b][:, cols],
                    in0=gates_of[j][:, 0:GROUP],
                    scalar1=EPS,
                    scalar2=None,
                    op0=ALU.max,
                    op1=ALU.add,
                    accum_out=group_sums[b][:, q : q + 1],
                )

            def turn():
                nc.scalar.copy(out=hi_by_expert[b][:, cols], in_=k_by_expert[b][:, cols])
                bank = banks.tile([P, BANK_WORDS], F32, name="bank")
                for c in range(GROUP_TILES):
                    at = q * GROUP + c * P
                    nc.tensor.transpose(
                        bank[:, c * P : (c + 1) * P], k_by_expert[b][:, at : at + P], identity[:]
                    )
                nc.scalar.copy(out=hi_by_token[b][:, cols], in_=bank[:, 0:GROUP])
                turned["bank"] = bank

            def split():
                for lo, whole, hi in (
                    (lo_by_expert, k_by_expert[b][:, cols], hi_by_expert),
                    (lo_by_token, turned["bank"][:, 0:GROUP], hi_by_token),
                ):
                    nc.vector.tensor_tensor(
                        out=lo[b][:, cols], in0=whole, in1=hi[b][:, cols], op=ALU.subtract
                    )

            return [clamp, turn, split]

        def pair_of_reciprocal(sums, width, name):
            whole = vectors.tile([P, width], F32, name=name + "_whole")
            nc.vector.reciprocal(out=whole[:], in_=sums)
            hi = whole[:].bitcast(BF16)[:, 1 : 2 * width : 2]
            lo = vectors.tile([P, width], BF16, name=name + "_lo")
            nc.vector.tensor_tensor(out=lo[:], in0=whole[:], in1=hi, op=ALU.subtract)
            return whole, hi, lo[:]

        def sinkhorn_steps(b, lone):
            state = {"products": 0}

            def next_repeat():
                state["products"] += 1
                state["repeat"] = LONE_REPEAT if state["products"] > 2 * ROUNDS - 1 - lone else REPEAT
                return state["repeat"]

            def nothing():
                return

            def first_token_step():
                column_sum = vectors.tile([P, 1], F32, name="column_sum%d" % b)
                nc.vector.reduce_sum(out=column_sum[:], in_=group_sums[b][:], axis=mybir.AxisListType.X)
                state["v"] = pair_of_reciprocal(column_sum[:], 1, "v%d" % b)

            def multiply_by_v():
                v_whole, v_hi, v_lo = state["v"]
                repeat = next_repeat()
                bank = banks.tile([P, BANK_WORDS], F32, name="bank")
                terms = []
                for matrix, vector in ((hi_by_expert, v_hi), (lo_by_expert, v_hi), (hi_by_expert, v_lo)):
                    for c in range(TILES_PER_BATCH):
                        terms.append((matrix, vector, c))
                for t in range(len(terms)):
                    matrix, vector, c = terms[t]
                    nc.tensor.matmul(
                        out=bank[:, c * repeat : (c + 1) * repeat],
                        lhsT=matrix[b][:, c * P : (c + 1) * P],
                        rhs=vector[:, 0:1].to_broadcast([P, repeat]),
                        start=(t == 0),
                        stop=(t == len(terms) - 1),
                    )
                state["bank"] = bank

            def take_u():
                repeat = state["repeat"]
                sums = state["bank"][:, 0 : TILES_PER_BATCH * repeat : repeat]
                state["u"] = pair_of_reciprocal(sums, TILES_PER_BATCH, "u%d" % b)

            def multiply_by_u():
                u_whole, u_hi, u_lo = state["u"]
                repeat = next_repeat()
                bank = banks.tile([P, BANK_WORDS], F32, name="bank")
                terms = []
                for matrix, vector in ((hi_by_token, u_hi), (lo_by_token, u_hi), (hi_by_token, u_lo)):
                    for c in range(TILES_PER_BATCH):
                        terms.append((matrix, vector, c))
                for t in range(len(terms)):
                    matrix, vector, c = terms[t]
                    nc.tensor.matmul(
                        out=bank[:, 0:repeat],
                        lhsT=matrix[b][:, c * P : (c + 1) * P],
                        rhs=vector[:, c : c + 1].to_broadcast([P, repeat]),
                        start=(t == 0),
                        stop=(t == len(terms) - 1),
                    )
                state["bank"] = bank

            def take_v():
                state["v"] = pair_of_reciprocal(state["bank"][:, 0:1], 1, "v%d" % b)

            def scale_by_v():
                v_whole, v_hi, v_lo = state["v"]
                repeat = state["repeat"]
                for h in range(OUT_HALVES):
                    cols = slice(h * OUT_COLS, (h + 1) * OUT_COLS)
                    scaled = keep.tile([P, OUT_COLS], F32, name="scaled%d%d" % (b, h))
                    nc.vector.tensor_scalar(
                        out=scaled[:], in0=k_by_expert[b][:, cols], scalar1=v_whole[:, 0:1], scalar2=None, op0=ALU.mult
                    )
                    state["scaled", h] = scaled
                u_whole = vectors.tile([P, TILES_PER_BATCH], F32, name="last_u%d" % b)
                nc.vector.reciprocal(
                    out=u_whole[:], in_=state["bank"][:, 0 : TILES_PER_BATCH * repeat : repeat]
                )
                state["u"] = u_whole

            def turn_scaled():
                for h in range(OUT_HALVES):
                    bank = banks.tile([P, BANK_WORDS], F32, name="bank")
                    for c in range(OUT_TILES):
                        at = slice(c * P, (c + 1) * P)
                        nc.tensor.transpose(bank[:, at], state["scaled", h][:, at], identity[:])
                    state["turned", h] = bank

            def result():
                for h in range(OUT_HALVES):
                    done = keep.tile([P, OUT_COLS], F32, name="result%d%d" % (b, h))
                    for c in range(OUT_TILES):
                        at = slice(c * P, (c + 1) * P)
                        u = state["u"][:, h * OUT_TILES + c : h * OUT_TILES + c + 1]
                        if h == 0:
                            nc.vector.tensor_scalar(
                                out=done[:, at], in0=state["turned", h][:, at], scalar1=u, scalar2=None, op0=ALU.mult
                            )
                        else:
                            nc.scalar.activation(
                                out=done[:, at], in_=state["turned", h][:, at], func=ACT.Copy, scale=u
                            )
                    rows = out[b].rearrange("(r h c) e -> h r (c e)", h=OUT_HALVES, c=OUT_TILES)
                    nc.sync.dma_start(out=rows[h], in_=done[:])

            steps = [(nothing, first_token_step)]
            for r in range(ROUNDS - 1):
                steps.append((multiply_by_v, take_u))
                steps.append((multiply_by_u, take_v))
            steps.append((multiply_by_v, scale_by_v))
            steps.append((turn_scaled, result))
            return steps

        chores = []
        chores_done = 0
        early_steps = sinkhorn_steps(0, 0)
        late_steps = sinkhorn_steps(1, EARLY_STEPS - 1)
        steps_done = 0
        multiplied = 0
        for i in range(len(units) + 2):
            ready = chores_done >= 3 * GROUPS_PER_BATCH and steps_done < EARLY_STEPS
            if chores_done < len(chores):
                chores[chores_done]()
                chores_done += 1
            if ready:
                early_steps[steps_done][0]()
            if i < len(units):
                transpose_unit(i)
            if ready:
                early_steps[steps_done][1]()
                steps_done += 1
            if 0 <= i - 1 < len(units):
                quantise_unit(i - 1)
            left = len(units) - i
            if (i % RUN == RUN - 1 or left <= SINGLE_RUNS) and left > LAST_UNITS or left <= 0:
                for m in range(multiplied, i - 1):
                    multiply_unit(m)
                multiplied = max(multiplied, i - 1)

        clamp, turn, split = chores[chores_done:]
        clamp()
        late_steps[0][1]()
        turn()
        split()
        for s in range(1, len(late_steps)):
            late_steps[s][0]()
            early = steps_done < len(early_steps)
            if early:
                early_steps[steps_done][0]()
            late_steps[s][1]()
            if early:
                early_steps[steps_done][1]()
                steps_done += 1
